import numpy as np
import ml_dtypes


def mxq(x, axis, fmt="e4m3"):
    dtype, down = {"e4m3": (ml_dtypes.float8_e4m3fn, 7), "e5m2": (ml_dtypes.float8_e5m2, 14)}[fmt]
    v = np.moveaxis(np.asarray(x, np.float32).astype(ml_dtypes.bfloat16).astype(np.float64), axis, -1)
    blocks = v.reshape(v.shape[:-1] + (-1, 32))
    amax = np.abs(blocks).max(-1, keepdims=True)
    byte = np.maximum(np.where(amax > 0, np.frexp(amax)[1] - 1 + 127, 0) - down, 1)
    scale = np.exp2(byte - 127.0)
    codes = (blocks / scale).astype(np.float32).astype(dtype).astype(np.float64)
    return np.moveaxis((codes * scale).reshape(v.shape), -1, axis)


WIDE = False


def mx_kscale(k):
    if not WIDE:
        return np.ones(k)
    levels = np.array([10, -10, 5, -5, 0])
    if k % 512:
        return np.exp2(np.random.permutation(np.resize(levels, k // 32))).repeat(32)
    a = np.empty((k // 512, 16))
    for p in range(k // 512):
        a[p, :8] = np.random.permutation(np.resize(levels, 8))
        for g in range(8):
            far = levels[np.abs(levels - a[p, g]) >= 10]
            a[p, g + 8] = far[np.random.randint(len(far))]
    return np.exp2(a.ravel()).repeat(32)


BF16 = ml_dtypes.bfloat16


def bf(x):
    return np.asarray(x, np.float32).astype(BF16)


def f64(x):
    return np.asarray(x).astype(np.float64)


B, H0, C0, C1, C2, NA, NO = 2, 32, 512, 512, 1024, 3, 128
H1, H2 = H0 // 2, H0 // 4
O = NA * NO


def sigmoid(v):
    return 1.0 / (1.0 + np.exp(-v))


def _draw_level(c, h):
    s = mx_kscale(c)
    f = bf(np.random.standard_normal((B, c, h, h)) * s[None, :, None, None])
    w = bf(np.random.standard_normal((O, c)) / np.sqrt(c) / s[None, :])
    b = bf(np.random.standard_normal(O) * 0.5)
    return f, w, b


def draw0():
    f0, w0, b0 = _draw_level(C0, H0)
    f1, w1, b1 = _draw_level(C1, H1)
    f2, w2, b2 = _draw_level(C2, H2)
    anchors = bf(1.0 + 4.0 * np.random.random((3, NA, 2)))
    return {"f0": f0, "f1": f1, "f2": f2, "w0": w0, "b0": b0, "w1": w1, "b1": b1, "w2": w2, "b2": b2, "anchors": anchors}


def _decode_level(f, w, b, anchors_i):
    nb, c, h, wd = f.shape
    y = (mxq(w, 1, "e4m3") @ mxq(f.reshape(nb, c, h * wd), 1, "e4m3")) + b[None, :, None]
    y = y.reshape(nb, NA, NO, h, wd).transpose(0, 1, 3, 4, 2)
    xy = 2.0 * sigmoid(y[..., 0:2]) - 0.5
    wh = np.square(2.0 * sigmoid(y[..., 2:4])) * anchors_i[None, :, None, None, :]
    rest = y[..., 4:]
    out = np.concatenate([xy, wh, rest], axis=-1)
    return out.reshape(nb, -1, NO)


def core(f0, f1, f2, w0, b0, w1, b1, w2, b2, anchors):
    a = f64(anchors)
    outs = [
        _decode_level(f64(f0), f64(w0), f64(b0), a[0]),
        _decode_level(f64(f1), f64(w1), f64(b1), a[1]),
        _decode_level(f64(f2), f64(w2), f64(b2), a[2]),
    ]
    return np.concatenate(outs, axis=1)


def e4m3fn_bytes(y):
    return np.clip(np.asarray(y, np.float64), -448.0, 448.0).astype(np.float32).astype(ml_dtypes.float8_e4m3fn).view(np.uint8)


def e4m3fn_values(b):
    return np.asarray(b, np.uint8).view(ml_dtypes.float8_e4m3fn).astype(np.float64)


def setup_inputs():
    d = draw0()
    x0 = np.asarray(d['f0']).astype(np.float64)
    s = (np.max(np.abs(x0), axis=(0, 2, 3), keepdims=True) / 448.0).astype(np.float32)
    out = {}
    for k, v in d.items():
        if k == 'f0':
            out['f0_bytes'] = e4m3fn_bytes(x0 / s.astype(np.float64))
            out['f0_scale'] = s
        else:
            out[k] = v
    return out


def reference(f0_bytes, f0_scale, f1, f2, w0, b0, w1, b1, w2, b2, anchors):
    return core(e4m3fn_values(f0_bytes) * f0_scale.astype(np.float64), f1, f2, w0, b0, w1, b1, w2, b2, anchors)

@@ -1,0 +1,270 @@
+from contextlib import ExitStack
+
+import concourse.mybir as mybir
+from concourse.masks import make_identity
+
+F32 = mybir.dt.float32
+BF16 = mybir.dt.bfloat16
+U32 = mybir.dt.uint32
+U8 = mybir.dt.uint8
+FP8 = mybir.dt.float8_e4m3fn
+FP8X4 = mybir.dt.float8_e4m3fn_x4
+ACT = mybir.ActivationFunctionType
+ALU = mybir.AluOpType
+
+P = 128
+NA = 3
+FLOPS = 2 * 384 * (512 * 2048 + 512 * 512 + 1024 * 128)
+
+WIDEN = ["SVVV", "SSVV", "SSSS", "SSSS"]
+INTERLEAVE = "VVVS"
+
+
+def tile_head_kernel(tc, f0_bytes, f0_scale, f1, f2, w0, b0, w1, b1, w2, b2, anchors, out):
+    nc = tc.nc
+    with ExitStack() as ctx:
+        keep = ctx.enter_context(tc.tile_pool(name="keep", bufs=1))
+        psum = ctx.enter_context(tc.psum_pool(name="psum", bufs=8))
+
+        zero1 = keep.tile([P, 1], F32, name="zero1")
+        nc.vector.memset(zero1[:], 0.0)
+        warm = keep.tile([P, 1], F32, name="warm")
+        nc.scalar.activation(out=warm[:], in_=zero1[:], func=ACT.Sigmoid)
+        ident = keep.tile([P, P], F32, name="ident")
+        make_identity(nc, ident[:])
+        ones = keep.tile([P, P], BF16, name="ones")
+        nc.vector.memset(ones[:], 1.0)
+        brow = keep.tile([P, 1184], BF16, name="brow")
+        nc.vector.memset(brow[:], 0.0)
+
+        f0v = [f0_bytes[n].rearrange("(p t) h w -> p t (h w)", t=4) for n in range(2)]
+        f0b_00 = keep.tile([P, 4, 512], U8, name="f0b_00")
+        nc.sync.dma_start(out=f0b_00[:], in_=f0v[0][:, :, 0:512])
+        sc = keep.tile([P, 4], F32, name="sc")
+        nc.sync.dma_start(out=sc[:], in_=f0_scale[0, :, 0, 0].rearrange("(p t) -> p t", t=4))
+        w0sb = keep.tile([P, NA, 512], BF16, name="w0sb")
+        nc.sync.dma_start(out=w0sb[:], in_=w0.rearrange("(a p) k -> p a k", p=P))
+        f0b_01 = keep.tile([P, 4, 512], U8, name="f0b_01")
+        nc.sync.dma_start(out=f0b_01[:], in_=f0v[0][:, :, 512:1024])
+        nc.sync.dma_start(out=brow[0:1, 0:384], in_=b0.unsqueeze(0))
+        nc.sync.dma_start(out=brow[0:1, 384:402], in_=anchors.rearrange("(o l) a j -> o (l a j)", o=1))
+        f0b_1 = keep.tile([P, 4, 1024], U8, name="f0b_1")
+        nc.sync.dma_start(out=f0b_1[:], in_=f0v[1])
+        w1sb = keep.tile([P, NA, 512], BF16, name="w1sb")
+        nc.sync.dma_start(out=w1sb[:], in_=w1.rearrange("(a p) k -> p a k", p=P))
+        f1sb = keep.tile([P, 2, 4, 256], BF16, name="f1sb")
+        nc.sync.dma_start(out=f1sb[:].rearrange("p n t c -> p n (t c)"),
+                          in_=f1.rearrange("n (p t) h w -> p n (t h w)", t=4))
+        w2sb = keep.tile([P, NA, 1024], BF16, name="w2sb")
+        nc.sync.dma_start(out=w2sb[:], in_=w2.rearrange("(a p) k -> p a k", p=P))
+        f2sb = keep.tile([P, 2, 2, 4, 64], BF16, name="f2sb")
+        for n in range(2):
+            nc.sync.dma_start(out=f2sb[:, n].rearrange("p g t c -> p g (t c)"),
+                              in_=f2[n].rearrange("(g p t) h w -> p g (t h w)", g=2, t=4))
+        nc.sync.dma_start(out=brow[0:1, 416:800], in_=b1.unsqueeze(0))
+        nc.sync.dma_start(out=brow[0:1, 800:1184], in_=b2.unsqueeze(0))
+        byte_src = [f0b_00[:], f0b_01[:], f0b_1[:, :, 0:512], f0b_1[:, :, 512:1024]]
+
+        bias = keep.tile([P, 1152], BF16, name="bias")
+        anc = keep.tile([P, 18], F32, name="anc")
+
+        def spread_bias0():
+            bb0 = psum.tile([P, 1024], BF16, tag="bank", name="bb0")
+            nc.tensor.matmul(out=bb0[:, 0:402], lhsT=ones[:], rhs=brow[:, 0:402], start=True, stop=True)
+            nc.scalar.copy(out=bias[:, 0:384], in_=bb0[:, 0:384])
+            nc.scalar.copy(out=anc[:], in_=bb0[:, 384:402])
+
+        def spread_bias12():
+            bb1 = psum.tile([P, 1024], BF16, tag="bank", name="bb1")
+            nc.tensor.matmul(out=bb1[:, 0:384], lhsT=ones[:], rhs=brow[:, 416:800], start=True, stop=True)
+            nc.tensor.matmul(out=bb1[:, 384:768], lhsT=ones[:], rhs=brow[:, 800:1184], start=True, stop=True)
+            nc.scalar.copy(out=bias[:, 384:1152], in_=bb1[:, 0:768])
+
+        def prep_weights(w_sb, n_pass, tagname):
+            n_units = NA * n_pass
+            grouped = keep.tile([P, n_units * 512], BF16, name="wg_" + tagname, align_bytes=64)
+            codes = keep.tile([P, n_units * P], U32, name="wc_" + tagname, align_bytes=64)
+            scales = keep.tile([P, n_units * P], U8, name="ws_" + tagname, align_bytes=64)
+            words = w_sb[:].bitcast(F32)
+            units = [(g, a) for g in range(n_pass) for a in range(NA)]
+            for first in range(0, n_units, 2):
+                pair = units[first:first + 2]
+                n = len(pair)
+                bank = psum.tile([P, 2, 2, P], F32, tag="bank", name="wt_%s_%d" % (tagname, first))
+                for s, (g, a) in enumerate(pair):
+                    for u in range(2):
+                        nc.tensor.transpose(bank[:, s, u, :], words[:, a, 256 * g + u:256 * (g + 1):2], ident[:])
+                nc.scalar.copy(
+                    out=grouped[:, first * 512:(first + n) * 512].bitcast(F32).rearrange(
+                        "p (s o u) -> p s o u", s=n, u=2),
+                    in_=bank[:, 0:n].rearrange("p s u o -> p s o u"))
+            return grouped, codes, scales
+
+        def quantize(grouped, codes, scales, widths):
+            c0 = 0
+            for wd in widths:
+                nc.vector.quantize_mx(out=codes[:, c0 // 4:(c0 + wd) // 4].bitcast(FP8X4),
+                                      scales=scales[:, c0 // 4:(c0 + wd) // 4],
+                                      in_=grouped[:, c0:c0 + wd])
+                c0 += wd
+
+        def feature_tiles(width, tagname):
+            grouped = keep.tile([P, width], BF16, name="fg_" + tagname, align_bytes=64)
+            codes = keep.tile([P, width // 4], U32, name="fc_" + tagname, align_bytes=64)
+            scales = keep.tile([P, width // 4], U8, name="fs_" + tagname, align_bytes=64)
+            return grouped, codes, scales
+
+        def chunk_matmuls(fc, fs, wc, ws, tagname):
+            banks = []
+            for a in range(NA):
+                bank = psum.tile([P, 4, P], F32, tag="bank", name="o_%s_%d" % (tagname, a))
+                for i in range(4):
+                    nc.tensor.matmul_mx(out=bank[:, i, :],
+                                        lhsT=fc[:, i * P:(i + 1) * P].bitcast(FP8X4),
+                                        lhsT_scale=fs[:, i * P:(i + 1) * P],
+                                        rhs=wc[:, a * P:(a + 1) * P].bitcast(FP8X4),
+                                        rhs_scale=ws[:, a * P:(a + 1) * P],
+                                        start=True, stop=True)
+                banks.append(bank)
+            return banks
+
+        def chunk_adds(banks, res, level):
+            for a in range(NA):
+                nc.vector.tensor_tensor(
+                    out=res[:, a], in0=banks[a][:],
+                    in1=bias[:, level * 384 + a * P:level * 384 + (a + 1) * P].unsqueeze(1).to_broadcast([P, 4, P]),
+                    op=ALU.add)
+
+        def decode(res, level, reps, tagname):
+            sig = keep.tile([P, NA, reps, 4], F32, name="sig_" + tagname)
+            sq = keep.tile([P, NA, reps, 2], F32, name="sq_" + tagname)
+            nc.scalar.activation(out=sig[:], in_=res[:, :, :, 0:4], func=ACT.Sigmoid)
+            nc.scalar.activation(out=res[:, :, :, 0:2], in_=sig[:, :, :, 0:2], func=ACT.Copy, scale=2.0, bias=-0.5)
+            nc.scalar.activation(out=sq[:], in_=sig[:, :, :, 2:4], func=ACT.Square, scale=2.0)
+            nc.vector.tensor_tensor(
+                out=res[:, :, :, 2:4], in0=sq[:],
+                in1=anc[:, level * 6:(level + 1) * 6].rearrange("p (a j) -> p a j", j=2).unsqueeze(2).to_broadcast(
+                    [P, NA, reps, 2]),
+                op=ALU.mult)
+
+        def anchors_of(level, a0, na, reps):
+            return anc[:, level * 6 + a0 * 2:level * 6 + (a0 + na) * 2].rearrange(
+                "p (a j) -> p a j", j=2).unsqueeze(2).to_broadcast([P, na, reps, 2])
+
+        def bank_first_fields(bank, res_a, level, a, reps, tagname):
+            b0c = level * 384 + a * P
+            d4 = keep.tile([P, 1, reps, 4], F32, name="d4_" + tagname)
+            sig = keep.tile([P, 1, reps, 4], F32, name="sg_" + tagname)
+            sq = keep.tile([P, 1, reps, 2], F32, name="sq_" + tagname)
+            nc.vector.tensor_tensor(out=d4[:, 0], in0=bank[:, :, 0:4],
+                                    in1=bias[:, b0c:b0c + 4].unsqueeze(1).to_broadcast([P, reps, 4]), op=ALU.add)
+            nc.scalar.activation(out=sig[:], in_=d4[:], func=ACT.Sigmoid)
+            nc.scalar.activation(out=sq[:], in_=sig[:, :, :, 2:4], func=ACT.Square, scale=2.0)
+            nc.scalar.activation(out=res_a[:, :, 0:2], in_=sig[:, 0, :, 0:2], func=ACT.Copy, scale=2.0, bias=-0.5)
+            nc.vector.tensor_tensor(out=res_a[:, :, 4:P], in0=bank[:, :, 4:P],
+                                    in1=bias[:, b0c + 4:b0c + P].unsqueeze(1).to_broadcast([P, reps, P - 4]),
+                                    op=ALU.add)
+            nc.vector.tensor_tensor(out=res_a[:, :, 2:4], in0=sq[:, 0], in1=anchors_of(level, a, 1, reps)[:, 0],
+                                    op=ALU.mult)
+
+        wide = [keep.tile([P, 4, 512], BF16, name="wide%d" % k) for k in range(4)]
+        f0q = [feature_tiles(2048, "l0_%d" % k) for k in range(4)]
+        res0 = [keep.tile([P, NA, 4, P], F32, name="res0_%d" % k) for k in range(4)]
+        out0 = [out[n, 0:3072, :].rearrange("(a c p i) j -> c p a (i j)", a=NA, c=2, p=P, i=4) for n in range(2)]
+
+        def widen(k):
+            for t in range(4):
+                src = byte_src[k][:, t, :].bitcast(FP8)
+                if WIDEN[k][t] == "S":
+                    nc.scalar.activation(out=wide[k][:, t, :], in_=src, func=ACT.Copy, scale=sc[:, t:t + 1])
+                else:
+                    nc.vector.tensor_scalar(out=wide[k][:, t, :], in0=src, scalar1=sc[:, t:t + 1], scalar2=None,
+                                            op0=ALU.mult)
+
+        def interleave0(k):
+            dst = f0q[k][0][:].rearrange("p (i m t) -> p i m t", i=4, t=4)
+            src = wide[k][:].rearrange("p t (m i) -> p i m t", i=4)
+            if INTERLEAVE[k] == "V":
+                nc.vector.tensor_copy(out=dst, in_=src)
+            else:
+                nc.scalar.copy(out=dst, in_=src)
+
+        def quantize0(k):
+            quantize(f0q[k][0], f0q[k][1], f0q[k][2], [2048])
+
+        def finish0(k, banks):
+            chunk_adds(banks, res0[k], 0)
+            decode(res0[k], 0, 4, "l0_%d" % k)
+            nc.sync.dma_start(out=out0[k // 2][k % 2], in_=res0[k][:].rearrange("p a i j -> p a (i j)"))
+
+        widen(0)
+        w0g, w0c, w0s = prep_weights(w0sb, 1, "w0")
+        interleave0(0)
+        widen(1)
+        quantize0(0)
+        quantize(w0g, w0c, w0s, [1024, 512])
+        spread_bias0()
+        banks = chunk_matmuls(f0q[0][1], f0q[0][2], w0c, w0s, "l0_0")
+        interleave0(1)
+        widen(2)
+        quantize0(1)
+        finish0(0, banks)
+        banks = chunk_matmuls(f0q[1][1], f0q[1][2], w0c, w0s, "l0_1")
+        interleave0(2)
+        widen(3)
+        quantize0(2)
+        finish0(1, banks)
+        banks = chunk_matmuls(f0q[2][1], f0q[2][2], w0c, w0s, "l0_2")
+        interleave0(3)
+        quantize0(3)
+        w1g, w1c, w1s = prep_weights(w1sb, 1, "w1")
+        f1g, f1c, f1s = feature_tiles(2048, "l1")
+        for n in range(2):
+            nc.scalar.copy(out=f1g[:, n * 1024:(n + 1) * 1024].rearrange("p (i m t) -> p i m t", i=2, t=4),
+                           in_=f1sb[:, n].rearrange("p t (m i) -> p i m t", i=2))
+        finish0(2, banks)
+        banks = chunk_matmuls(f0q[3][1], f0q[3][2], w0c, w0s, "l0_3")
+        quantize(w1g, w1c, w1s, [1024, 512])
+        quantize(f1g, f1c, f1s, [2048])
+        w2g, w2c, w2s = prep_weights(w2sb, 2, "w2")
+        f2g, f2c, f2s = feature_tiles(1024, "l2")
+        for g in range(2):
+            nc.scalar.copy(out=f2g[:, g * 512:(g + 1) * 512].rearrange("p (n c t) -> p n c t", n=2, t=4),
+                           in_=f2sb[:, :, g].rearrange("p n t c -> p n c t"))
+        spread_bias12()
+        finish0(3, banks)
+        quantize(w2g, w2c, w2s, [2048, 1024])
+        quantize(f2g, f2c, f2s, [1024])
+
+        res1 = keep.tile([P, NA, 4, P], F32, name="res1")
+        banks = chunk_matmuls(f1c, f1s, w1c, w1s, "l1")
+        out1 = out[:, 3072:3840, :].rearrange("n (a p i) j -> a p n (i j)", a=NA, i=2)
+        for a in range(NA):
+            bank_first_fields(banks[a], res1[:, a], 1, a, 4, "l1_%d" % a)
+            nc.sync.dma_start(out=out1[a], in_=res1[:, a].rearrange("p (n i) j -> p n (i j)", n=2))
+
+        res2 = keep.tile([P, NA, P], F32, name="res2")
+        bank2 = psum.tile([P, NA, P], F32, tag="bank", name="o_l2")
+        for a in range(NA):
+            for g in range(2):
+                q = g * NA + a
+                nc.tensor.matmul_mx(out=bank2[:, a, :],
+                                    lhsT=f2c[:, g * P:(g + 1) * P].bitcast(FP8X4),
+                                    lhsT_scale=f2s[:, g * P:(g + 1) * P],
+                                    rhs=w2c[:, q * P:(q + 1) * P].bitcast(FP8X4),
+                                    rhs_scale=w2s[:, q * P:(q + 1) * P],
+                                    start=(g == 0), stop=(g == 1))
+        bias2 = bias[:, 768:1152].rearrange("p (a j) -> p a j", a=NA)
+        d4 = keep.tile([P, NA, 4], F32, name="d4_l2")
+        sig = keep.tile([P, NA, 4], F32, name="sg_l2")
+        sq = keep.tile([P, NA, 2], F32, name="sq_l2")
+        nc.vector.tensor_tensor(out=d4[:], in0=bank2[:, :, 0:4], in1=bias2[:, :, 0:4], op=ALU.add)
+        nc.scalar.activation(out=sig[:], in_=d4[:], func=ACT.Sigmoid)
+        nc.scalar.activation(out=sq[:], in_=sig[:, :, 2:4], func=ACT.Square, scale=2.0)
+        nc.scalar.activation(out=res2[:, :, 0:2], in_=sig[:, :, 0:2], func=ACT.Copy, scale=2.0, bias=-0.5)
+        nc.vector.tensor_tensor(out=res2[:, :, 4:P], in0=bank2[:, :, 4:P], in1=bias2[:, :, 4:P], op=ALU.add)
+        nc.vector.tensor_tensor(out=res2[:, :, 2:4], in0=sq[:],
+                                in1=anc[:, 12:18].rearrange("p (a j) -> p a j", j=2), op=ALU.mult)
+        for n in range(2):
+            nc.sync.dma_start(out=out[n, 3840:4032, :].rearrange("(a c) j -> c a j", a=NA),
+                              in_=res2[n * 64:(n + 1) * 64, :, :])

@@ -16,8 +16,7 @@ P = 128
 NA = 3
 FLOPS = 2 * 384 * (512 * 2048 + 512 * 512 + 1024 * 128)
 
-WIDEN = ["SVVV", "SSVV", "SSSS", "SSSS"]
-INTERLEAVE = "VVVS"
+PERM = [False, False, False, True]
 
 
 def tile_head_kernel(tc, f0_bytes, f0_scale, f1, f2, w0, b0, w1, b1, w2, b2, anchors, out):
@@ -25,6 +24,7 @@ def tile_head_kernel(tc, f0_bytes, f0_scale, f1, f2, w0, b0, w1, b1, w2, b2, anc
     with ExitStack() as ctx:
         keep = ctx.enter_context(tc.tile_pool(name="keep", bufs=1))
         psum = ctx.enter_context(tc.psum_pool(name="psum", bufs=8))
+        ctx.enter_context(tc.manual_schedule())
 
         zero1 = keep.tile([P, 1], F32, name="zero1")
         nc.vector.memset(zero1[:], 0.0)
@@ -36,6 +36,10 @@ def tile_head_kernel(tc, f0_bytes, f0_scale, f1, f2, w0, b0, w1, b1, w2, b2, anc
         nc.vector.memset(ones[:], 1.0)
         brow = keep.tile([P, 1184], BF16, name="brow")
         nc.vector.memset(brow[:], 0.0)
+        nc.gpsimd.dma_start(out=brow[0:1, 0:384], in_=b0.unsqueeze(0))
+        nc.gpsimd.dma_start(out=brow[0:1, 384:402], in_=anchors.rearrange("(o l) a j -> o (l a j)", o=1))
+        nc.gpsimd.dma_start(out=brow[0:1, 416:800], in_=b1.unsqueeze(0))
+        nc.gpsimd.dma_start(out=brow[0:1, 800:1184], in_=b2.unsqueeze(0))
 
         f0v = [f0_bytes[n].rearrange("(p t) h w -> p t (h w)", t=4) for n in range(2)]
         f0b_00 = keep.tile([P, 4, 512], U8, name="f0b_00")
@@ -46,204 +50,257 @@ def tile_head_kernel(tc, f0_bytes, f0_scale, f1, f2, w0, b0, w1, b1, w2, b2, anc
         nc.sync.dma_start(out=w0sb[:], in_=w0.rearrange("(a p) k -> p a k", p=P))
         f0b_01 = keep.tile([P, 4, 512], U8, name="f0b_01")
         nc.sync.dma_start(out=f0b_01[:], in_=f0v[0][:, :, 512:1024])
-        nc.sync.dma_start(out=brow[0:1, 0:384], in_=b0.unsqueeze(0))
-        nc.sync.dma_start(out=brow[0:1, 384:402], in_=anchors.rearrange("(o l) a j -> o (l a j)", o=1))
         f0b_1 = keep.tile([P, 4, 1024], U8, name="f0b_1")
         nc.sync.dma_start(out=f0b_1[:], in_=f0v[1])
-        w1sb = keep.tile([P, NA, 512], BF16, name="w1sb")
-        nc.sync.dma_start(out=w1sb[:], in_=w1.rearrange("(a p) k -> p a k", p=P))
         f1sb = keep.tile([P, 2, 4, 256], BF16, name="f1sb")
         nc.sync.dma_start(out=f1sb[:].rearrange("p n t c -> p n (t c)"),
                           in_=f1.rearrange("n (p t) h w -> p n (t h w)", t=4))
+        w1sb = keep.tile([P, NA, 512], BF16, name="w1sb")
+        nc.sync.dma_start(out=w1sb[:], in_=w1.rearrange("(a p) k -> p a k", p=P))
         w2sb = keep.tile([P, NA, 1024], BF16, name="w2sb")
         nc.sync.dma_start(out=w2sb[:], in_=w2.rearrange("(a p) k -> p a k", p=P))
         f2sb = keep.tile([P, 2, 2, 4, 64], BF16, name="f2sb")
         for n in range(2):
             nc.sync.dma_start(out=f2sb[:, n].rearrange("p g t c -> p g (t c)"),
                               in_=f2[n].rearrange("(g p t) h w -> p g (t h w)", g=2, t=4))
-        nc.sync.dma_start(out=brow[0:1, 416:800], in_=b1.unsqueeze(0))
-        nc.sync.dma_start(out=brow[0:1, 800:1184], in_=b2.unsqueeze(0))
         byte_src = [f0b_00[:], f0b_01[:], f0b_1[:, :, 0:512], f0b_1[:, :, 512:1024]]
 
         bias = keep.tile([P, 1152], BF16, name="bias")
         anc = keep.tile([P, 18], F32, name="anc")
 
-        def spread_bias0():
-            bb0 = psum.tile([P, 1024], BF16, tag="bank", name="bb0")
-            nc.tensor.matmul(out=bb0[:, 0:402], lhsT=ones[:], rhs=brow[:, 0:402], start=True, stop=True)
-            nc.scalar.copy(out=bias[:, 0:384], in_=bb0[:, 0:384])
-            nc.scalar.copy(out=anc[:], in_=bb0[:, 384:402])
-
-        def spread_bias12():
-            bb1 = psum.tile([P, 1024], BF16, tag="bank", name="bb1")
-            nc.tensor.matmul(out=bb1[:, 0:384], lhsT=ones[:], rhs=brow[:, 416:800], start=True, stop=True)
-            nc.tensor.matmul(out=bb1[:, 384:768], lhsT=ones[:], rhs=brow[:, 800:1184], start=True, stop=True)
-            nc.scalar.copy(out=bias[:, 384:1152], in_=bb1[:, 0:768])
-
-        def prep_weights(w_sb, n_pass, tagname):
-            n_units = NA * n_pass
-            grouped = keep.tile([P, n_units * 512], BF16, name="wg_" + tagname, align_bytes=64)
-            codes = keep.tile([P, n_units * P], U32, name="wc_" + tagname, align_bytes=64)
-            scales = keep.tile([P, n_units * P], U8, name="ws_" + tagname, align_bytes=64)
-            words = w_sb[:].bitcast(F32)
-            units = [(g, a) for g in range(n_pass) for a in range(NA)]
-            for first in range(0, n_units, 2):
-                pair = units[first:first + 2]
-                n = len(pair)
-                bank = psum.tile([P, 2, 2, P], F32, tag="bank", name="wt_%s_%d" % (tagname, first))
-                for s, (g, a) in enumerate(pair):
-                    for u in range(2):
-                        nc.tensor.transpose(bank[:, s, u, :], words[:, a, 256 * g + u:256 * (g + 1):2], ident[:])
-                nc.scalar.copy(
-                    out=grouped[:, first * 512:(first + n) * 512].bitcast(F32).rearrange(
-                        "p (s o u) -> p s o u", s=n, u=2),
-                    in_=bank[:, 0:n].rearrange("p s u o -> p s o u"))
+        def mx_tiles(width, tagname):
+            grouped = keep.tile([P, width], BF16, name="g_" + tagname, align_bytes=64)
+            codes = keep.tile([P, width // 4], U32, name="c_" + tagname, align_bytes=64)
+            scales = keep.tile([P, width // 4], U8, name="s_" + tagname, align_bytes=64)
             return grouped, codes, scales
 
-        def quantize(grouped, codes, scales, widths):
-            c0 = 0
-            for wd in widths:
-                nc.vector.quantize_mx(out=codes[:, c0 // 4:(c0 + wd) // 4].bitcast(FP8X4),
-                                      scales=scales[:, c0 // 4:(c0 + wd) // 4],
-                                      in_=grouped[:, c0:c0 + wd])
-                c0 += wd
-
-        def feature_tiles(width, tagname):
-            grouped = keep.tile([P, width], BF16, name="fg_" + tagname, align_bytes=64)
-            codes = keep.tile([P, width // 4], U32, name="fc_" + tagname, align_bytes=64)
-            scales = keep.tile([P, width // 4], U8, name="fs_" + tagname, align_bytes=64)
-            return grouped, codes, scales
-
-        def chunk_matmuls(fc, fs, wc, ws, tagname):
-            banks = []
-            for a in range(NA):
-                bank = psum.tile([P, 4, P], F32, tag="bank", name="o_%s_%d" % (tagname, a))
-                for i in range(4):
-                    nc.tensor.matmul_mx(out=bank[:, i, :],
-                                        lhsT=fc[:, i * P:(i + 1) * P].bitcast(FP8X4),
-                                        lhsT_scale=fs[:, i * P:(i + 1) * P],
-                                        rhs=wc[:, a * P:(a + 1) * P].bitcast(FP8X4),
-                                        rhs_scale=ws[:, a * P:(a + 1) * P],
-                                        start=True, stop=True)
-                banks.append(bank)
-            return banks
-
-        def chunk_adds(banks, res, level):
-            for a in range(NA):
-                nc.vector.tensor_tensor(
-                    out=res[:, a], in0=banks[a][:],
-                    in1=bias[:, level * 384 + a * P:level * 384 + (a + 1) * P].unsqueeze(1).to_broadcast([P, 4, P]),
-                    op=ALU.add)
-
-        def decode(res, level, reps, tagname):
-            sig = keep.tile([P, NA, reps, 4], F32, name="sig_" + tagname)
-            sq = keep.tile([P, NA, reps, 2], F32, name="sq_" + tagname)
-            nc.scalar.activation(out=sig[:], in_=res[:, :, :, 0:4], func=ACT.Sigmoid)
-            nc.scalar.activation(out=res[:, :, :, 0:2], in_=sig[:, :, :, 0:2], func=ACT.Copy, scale=2.0, bias=-0.5)
-            nc.scalar.activation(out=sq[:], in_=sig[:, :, :, 2:4], func=ACT.Square, scale=2.0)
-            nc.vector.tensor_tensor(
-                out=res[:, :, :, 2:4], in0=sq[:],
-                in1=anc[:, level * 6:(level + 1) * 6].rearrange("p (a j) -> p a j", j=2).unsqueeze(2).to_broadcast(
-                    [P, NA, reps, 2]),
-                op=ALU.mult)
-
-        def anchors_of(level, a0, na, reps):
-            return anc[:, level * 6 + a0 * 2:level * 6 + (a0 + na) * 2].rearrange(
-                "p (a j) -> p a j", j=2).unsqueeze(2).to_broadcast([P, na, reps, 2])
-
-        def bank_first_fields(bank, res_a, level, a, reps, tagname):
-            b0c = level * 384 + a * P
-            d4 = keep.tile([P, 1, reps, 4], F32, name="d4_" + tagname)
-            sig = keep.tile([P, 1, reps, 4], F32, name="sg_" + tagname)
-            sq = keep.tile([P, 1, reps, 2], F32, name="sq_" + tagname)
-            nc.vector.tensor_tensor(out=d4[:, 0], in0=bank[:, :, 0:4],
-                                    in1=bias[:, b0c:b0c + 4].unsqueeze(1).to_broadcast([P, reps, 4]), op=ALU.add)
-            nc.scalar.activation(out=sig[:], in_=d4[:], func=ACT.Sigmoid)
-            nc.scalar.activation(out=sq[:], in_=sig[:, :, :, 2:4], func=ACT.Square, scale=2.0)
-            nc.scalar.activation(out=res_a[:, :, 0:2], in_=sig[:, 0, :, 0:2], func=ACT.Copy, scale=2.0, bias=-0.5)
-            nc.vector.tensor_tensor(out=res_a[:, :, 4:P], in0=bank[:, :, 4:P],
-                                    in1=bias[:, b0c + 4:b0c + P].unsqueeze(1).to_broadcast([P, reps, P - 4]),
-                                    op=ALU.add)
-            nc.vector.tensor_tensor(out=res_a[:, :, 2:4], in0=sq[:, 0], in1=anchors_of(level, a, 1, reps)[:, 0],
-                                    op=ALU.mult)
-
-        wide = [keep.tile([P, 4, 512], BF16, name="wide%d" % k) for k in range(4)]
-        f0q = [feature_tiles(2048, "l0_%d" % k) for k in range(4)]
+        wq = [mx_tiles(1536, "w0"), mx_tiles(1536, "w1"), mx_tiles(3072, "w2")]
+        wsb = [w0sb, w1sb, w2sb]
+        wide = [keep.tile([P, 4, 512], BF16, name="wide%d" % k, tag=("ovA" if k == 1 else "wide%d" % k),
+                          align_bytes=64) for k in range(4)]
+        f0q = [mx_tiles(2048, "f0_%d" % k) for k in range(4)]
+        f1c = keep.tile([P, 512], U32, name="c_f1", align_bytes=64)
+        f1s = keep.tile([P, 512], U8, name="s_f1", align_bytes=64)
+        f2c = keep.tile([P, 256], U32, name="c_f2", align_bytes=64)
+        f2s = keep.tile([P, 256], U8, name="s_f2", align_bytes=64)
         res0 = [keep.tile([P, NA, 4, P], F32, name="res0_%d" % k) for k in range(4)]
-        out0 = [out[n, 0:3072, :].rearrange("(a c p i) j -> c p a (i j)", a=NA, c=2, p=P, i=4) for n in range(2)]
+        res1 = keep.tile([P, NA, 4, P], F32, name="res1")
+        res2 = keep.tile([P, NA, P], F32, name="res2")
+        live = {}
 
-        def widen(k):
-            for t in range(4):
-                src = byte_src[k][:, t, :].bitcast(FP8)
-                if WIDEN[k][t] == "S":
-                    nc.scalar.activation(out=wide[k][:, t, :], in_=src, func=ACT.Copy, scale=sc[:, t:t + 1])
-                else:
-                    nc.vector.tensor_scalar(out=wide[k][:, t, :], in0=src, scalar1=sc[:, t:t + 1], scalar2=None,
-                                            op0=ALU.mult)
+        def widen(k, t, eng):
+            src = byte_src[k][:, t, :].bitcast(FP8)
+            if eng == "S":
+                nc.scalar.activation(out=wide[k][:, t, :], in_=src, func=ACT.Copy, scale=sc[:, t:t + 1])
+            else:
+                nc.vector.tensor_scalar(out=wide[k][:, t, :], in0=src, scalar1=sc[:, t:t + 1], scalar2=None,
+                                        op0=ALU.mult)
 
-        def interleave0(k):
-            dst = f0q[k][0][:].rearrange("p (i m t) -> p i m t", i=4, t=4)
-            src = wide[k][:].rearrange("p t (m i) -> p i m t", i=4)
-            if INTERLEAVE[k] == "V":
+        def interleave0(k, eng):
+            if PERM[k]:
+                dst = f0q[k][0][:].rearrange("p (i m t) -> p i m t", i=4, t=4)
+                src = wide[k][:].rearrange("p t (m i) -> p i m t", i=4)
+            else:
+                dst = f0q[k][0][:].rearrange("p (c t) -> p c t", t=4)
+                src = wide[k][:].rearrange("p t c -> p c t")
+            if eng == "V":
                 nc.vector.tensor_copy(out=dst, in_=src)
             else:
                 nc.scalar.copy(out=dst, in_=src)
 
-        def quantize0(k):
-            quantize(f0q[k][0], f0q[k][1], f0q[k][2], [2048])
+        def quantize(q3, c0, wd):
+            nc.vector.quantize_mx(out=q3[1][:, c0 // 4:(c0 + wd) // 4].bitcast(FP8X4),
+                                  scales=q3[2][:, c0 // 4:(c0 + wd) // 4],
+                                  in_=q3[0][:, c0:c0 + wd])
 
-        def finish0(k, banks):
-            chunk_adds(banks, res0[k], 0)
-            decode(res0[k], 0, 4, "l0_%d" % k)
-            nc.sync.dma_start(out=out0[k // 2][k % 2], in_=res0[k][:].rearrange("p a i j -> p a (i j)"))
+        def w_transposes(level, first, n):
+            words = wsb[level][:].bitcast(F32)
+            bank = psum.tile([P, 2, 2, P], F32, tag="bank", name="wt_%d_%d" % (level, first))
+            for s in range(n):
+                g, a = divmod(first + s, NA)
+                for u in range(2):
+                    nc.tensor.transpose(bank[:, s, u, :], words[:, a, 256 * g + u:256 * (g + 1):2], ident[:])
+            live["wt", level, first] = bank
 
-        widen(0)
-        w0g, w0c, w0s = prep_weights(w0sb, 1, "w0")
-        interleave0(0)
-        widen(1)
-        quantize0(0)
-        quantize(w0g, w0c, w0s, [1024, 512])
-        spread_bias0()
-        banks = chunk_matmuls(f0q[0][1], f0q[0][2], w0c, w0s, "l0_0")
-        interleave0(1)
-        widen(2)
-        quantize0(1)
-        finish0(0, banks)
-        banks = chunk_matmuls(f0q[1][1], f0q[1][2], w0c, w0s, "l0_1")
-        interleave0(2)
-        widen(3)
-        quantize0(2)
-        finish0(1, banks)
-        banks = chunk_matmuls(f0q[2][1], f0q[2][2], w0c, w0s, "l0_2")
-        interleave0(3)
-        quantize0(3)
-        w1g, w1c, w1s = prep_weights(w1sb, 1, "w1")
-        f1g, f1c, f1s = feature_tiles(2048, "l1")
-        for n in range(2):
-            nc.scalar.copy(out=f1g[:, n * 1024:(n + 1) * 1024].rearrange("p (i m t) -> p i m t", i=2, t=4),
-                           in_=f1sb[:, n].rearrange("p t (m i) -> p i m t", i=2))
-        finish0(2, banks)
-        banks = chunk_matmuls(f0q[3][1], f0q[3][2], w0c, w0s, "l0_3")
-        quantize(w1g, w1c, w1s, [1024, 512])
-        quantize(f1g, f1c, f1s, [2048])
-        w2g, w2c, w2s = prep_weights(w2sb, 2, "w2")
-        f2g, f2c, f2s = feature_tiles(1024, "l2")
-        for g in range(2):
-            nc.scalar.copy(out=f2g[:, g * 512:(g + 1) * 512].rearrange("p (n c t) -> p n c t", n=2, t=4),
-                           in_=f2sb[:, :, g].rearrange("p n t c -> p n c t"))
-        spread_bias12()
-        finish0(3, banks)
-        quantize(w2g, w2c, w2s, [2048, 1024])
-        quantize(f2g, f2c, f2s, [1024])
+        def w_empty(level, first, n):
+            bank = live["wt", level, first]
+            nc.scalar.copy(
+                out=wq[level][0][:, first * 512:(first + n) * 512].bitcast(F32).rearrange(
+                    "p (s o u) -> p s o u", s=n, u=2),
+                in_=bank[:, 0:n].rearrange("p s u o -> p s o u"))
 
-        res1 = keep.tile([P, NA, 4, P], F32, name="res1")
-        banks = chunk_matmuls(f1c, f1s, w1c, w1s, "l1")
+        def bias0_matmul():
+            bb = psum.tile([P, 1024], BF16, tag="bank", name="bb0")
+            nc.tensor.matmul(out=bb[:, 0:402], lhsT=ones[:], rhs=brow[:, 0:402], start=True, stop=True)
+            live["bb0"] = bb
+
+        def bias0_empty():
+            nc.scalar.copy(out=bias[:, 0:384], in_=live["bb0"][:, 0:384])
+            nc.scalar.copy(out=anc[:], in_=live["bb0"][:, 384:402])
+
+        def bias12_matmul():
+            bb = psum.tile([P, 1024], BF16, tag="bank", name="bb1")
+            nc.tensor.matmul(out=bb[:, 0:384], lhsT=ones[:], rhs=brow[:, 416:800], start=True, stop=True)
+            nc.tensor.matmul(out=bb[:, 384:768], lhsT=ones[:], rhs=brow[:, 800:1184], start=True, stop=True)
+            live["bb1"] = bb
+
+        def bias12_empty():
+            nc.scalar.copy(out=bias[:, 384:1152], in_=live["bb1"][:, 0:768])
+
+        def matmuls(tagname, fq, level):
+            for a in range(NA):
+                bank = psum.tile([P, 4, P], F32, tag="bank", name="o_%s_%d" % (tagname, a))
+                for i in range(4):
+                    nc.tensor.matmul_mx(out=bank[:, i, :],
+                                        lhsT=fq[1][:, i * P:(i + 1) * P].bitcast(FP8X4),
+                                        lhsT_scale=fq[2][:, i * P:(i + 1) * P],
+                                        rhs=wq[level][1][:, a * P:(a + 1) * P].bitcast(FP8X4),
+                                        rhs_scale=wq[level][2][:, a * P:(a + 1) * P],
+                                        start=True, stop=True)
+                live["o", tagname, a] = bank
+
+        def add0(k, a):
+            nc.vector.tensor_tensor(out=res0[k][:, a], in0=live["o", k, a][:],
+                                    in1=bias[:, a * P:(a + 1) * P].unsqueeze(1).to_broadcast([P, 4, P]), op=ALU.add)
+
+        def decode0_scalar(k):
+            sig = keep.tile([P, NA, 4, 4], F32, name="sig0_%d" % k)
+            sq = keep.tile([P, NA, 4, 2], F32, name="sq0_%d" % k, tag=["ovB", "ovC", "sq0_2", "sq0_3"][k], align_bytes=64)
+            nc.scalar.activation(out=sig[:], in_=res0[k][:, :, :, 0:4], func=ACT.Sigmoid)
+            nc.scalar.activation(out=sq[:], in_=sig[:, :, :, 2:4], func=ACT.Square, scale=2.0)
+            nc.scalar.activation(out=res0[k][:, :, :, 0:2], in_=sig[:, :, :, 0:2], func=ACT.Copy, scale=2.0, bias=-0.5)
+            live["sq", k] = sq
+
+        def decode0_vector(k):
+            nc.vector.tensor_tensor(
+                out=res0[k][:, :, :, 2:4], in0=live["sq", k][:],
+                in1=anc[:, 0:6].rearrange("p (a j) -> p a j", j=2).unsqueeze(2).to_broadcast([P, NA, 4, 2]),
+                op=ALU.mult)
+
+        def store0(k):
+            n, c = divmod(k, 2)
+            if PERM[k]:
+                nc.sync.dma_start(
+                    out=out[n, 0:3072, :].rearrange("(a c p i) j -> c p a (i j)", a=NA, c=2, p=P, i=4)[c],
+                    in_=res0[k][:].rearrange("p a i j -> p a (i j)"))
+            else:
+                for a in range(NA):
+                    r0 = a * 1024 + c * 512
+                    nc.sync.dma_start(out=out[n, r0:r0 + 512, :].rearrange("(i p) j -> p i j", p=P),
+                                      in_=res0[k][:, a])
+
+        def fields_add(tagname, bank, bias_ap):
+            d4 = keep.tile(list(bias_ap.shape), F32, name="d4_" + tagname)
+            nc.vector.tensor_tensor(out=d4[:], in0=bank[:, :, 0:4], in1=bias_ap, op=ALU.add)
+            live["d4", tagname] = d4
+
+        def fields_scalar(tagname, res_ap):
+            d4 = live["d4", tagname]
+            reps = d4.shape[1]
+            sig = keep.tile([P, reps, 4], F32, name="sg_" + tagname)
+            sq = keep.tile([P, reps, 2], F32, name="sq_" + tagname)
+            nc.scalar.activation(out=sig[:], in_=d4[:], func=ACT.Sigmoid)
+            nc.scalar.activation(out=sq[:], in_=sig[:, :, 2:4], func=ACT.Square, scale=2.0)
+            nc.scalar.activation(out=res_ap[:, :, 0:2], in_=sig[:, :, 0:2], func=ACT.Copy, scale=2.0, bias=-0.5)
+            live["sq", tagname] = sq
+
+        def bias1(a, j0, j1):
+            return bias[:, 384 + a * P + j0:384 + a * P + j1].unsqueeze(1).to_broadcast([P, 4, j1 - j0])
+
+        bias2 = bias[:, 768:1152].rearrange("p (a j) -> p a j", a=NA)
         out1 = out[:, 3072:3840, :].rearrange("n (a p i) j -> a p n (i j)", a=NA, i=2)
-        for a in range(NA):
-            bank_first_fields(banks[a], res1[:, a], 1, a, 4, "l1_%d" % a)
-            nc.sync.dma_start(out=out1[a], in_=res1[:, a].rearrange("p (n i) j -> p n (i j)", n=2))
 
-        res2 = keep.tile([P, NA, P], F32, name="res2")
+        def gpsimd_interleave(dst, src):
+            nc.gpsimd.tensor_scalar(out=dst, in0=src, scalar1=1.0, scalar2=0.0, op0=ALU.mult, op1=ALU.add)
+
+        def interleave1(n, tagname):
+            g = keep.tile([P, 1024], BF16, name="g_f1_%d" % n, tag=tagname, align_bytes=64)
+            gpsimd_interleave(g[:].rearrange("p (i m t) -> p i m t", i=2, t=4),
+                              f1sb[:, n].rearrange("p t (m i) -> p i m t", i=2))
+            live["g_f1", n] = g
+
+        def quantize1(n):
+            quantize((live["g_f1", n], f1c[:, n * 256:(n + 1) * 256], f1s[:, n * 256:(n + 1) * 256]), 0, 1024)
+
+        widen(0, 0, "S")
+        widen(0, 1, "V")
+        widen(0, 2, "V")
+        widen(0, 3, "V")
+        w_transposes(0, 0, 2)
+        w_transposes(0, 2, 1)
+        interleave0(0, "V")
+        widen(1, 0, "S")
+        widen(1, 1, "S")
+        w_empty(0, 0, 2)
+        w_empty(0, 2, 1)
+        widen(1, 2, "V")
+        widen(1, 3, "V")
+        quantize(f0q[0], 0, 2048)
+        quantize(wq[0], 0, 1024)
+        quantize(wq[0], 1024, 512)
+        bias0_matmul()
+        bias0_empty()
+        matmuls(0, f0q[0], 0)
+        for t in range(4):
+            widen(2, t, "S")
+        interleave0(1, "V")
+        interleave1(0, "ovA")
+        for a in range(NA):
+            add0(0, a)
+        quantize(f0q[1], 0, 2048)
+        matmuls(1, f0q[1], 0)
+        w_transposes(1, 0, 2)
+        w_transposes(1, 2, 1)
+        w_transposes(2, 0, 2)
+        w_transposes(2, 2, 2)
+        w_transposes(2, 4, 2)
+        for t in range(3):
+            widen(3, t, "S")
+        decode0_scalar(0)
+        widen(3, 3, "S")
+        interleave0(2, "V")
+        decode0_vector(0)
+        store0(0)
+        interleave1(1, "ovB")
+        for a in range(NA):
+            add0(1, a)
+        quantize(f0q[2], 0, 2048)
+        matmuls(2, f0q[2], 0)
+        interleave0(3, "S")
+        decode0_scalar(1)
+        quantize1(0)
+        quantize1(1)
+        decode0_vector(1)
+        store0(1)
+        f2g = keep.tile([P, 1024], BF16, name="g_f2", tag="ovC", align_bytes=64)
+        for g in range(2):
+            gpsimd_interleave(f2g[:, g * 512:(g + 1) * 512].rearrange("p (n c t) -> p n c t", n=2, t=4),
+                              f2sb[:, :, g].rearrange("p n t c -> p n c t"))
+        for a in range(NA):
+            add0(2, a)
+        quantize(f0q[3], 0, 2048)
+        w_empty(1, 0, 2)
+        w_empty(1, 2, 1)
+        w_empty(2, 0, 2)
+        w_empty(2, 2, 2)
+        w_empty(2, 4, 2)
+        bias12_matmul()
+        matmuls(3, f0q[3], 0)
+        decode0_scalar(2)
+        quantize(wq[1], 0, 1024)
+        quantize(wq[1], 1024, 512)
+        decode0_vector(2)
+        store0(2)
+        for a in range(NA):
+            add0(3, a)
+        matmuls("l1", (None, f1c, f1s), 1)
+        bias12_empty()
+        decode0_scalar(3)
+        quantize(wq[2], 0, 2048)
+        decode0_vector(3)
+        store0(3)
+        quantize(wq[2], 2048, 1024)
+        quantize((f2g, f2c, f2s), 0, 1024)
         bank2 = psum.tile([P, NA, P], F32, tag="bank", name="o_l2")
         for a in range(NA):
             for g in range(2):
@@ -251,19 +308,24 @@ def tile_head_kernel(tc, f0_bytes, f0_scale, f1, f2, w0, b0, w1, b1, w2, b2, anc
                 nc.tensor.matmul_mx(out=bank2[:, a, :],
                                     lhsT=f2c[:, g * P:(g + 1) * P].bitcast(FP8X4),
                                     lhsT_scale=f2s[:, g * P:(g + 1) * P],
-                                    rhs=w2c[:, q * P:(q + 1) * P].bitcast(FP8X4),
-                                    rhs_scale=w2s[:, q * P:(q + 1) * P],
+                                    rhs=wq[2][1][:, q * P:(q + 1) * P].bitcast(FP8X4),
+                                    rhs_scale=wq[2][2][:, q * P:(q + 1) * P],
                                     start=(g == 0), stop=(g == 1))
-        bias2 = bias[:, 768:1152].rearrange("p (a j) -> p a j", a=NA)
-        d4 = keep.tile([P, NA, 4], F32, name="d4_l2")
-        sig = keep.tile([P, NA, 4], F32, name="sg_l2")
-        sq = keep.tile([P, NA, 2], F32, name="sq_l2")
-        nc.vector.tensor_tensor(out=d4[:], in0=bank2[:, :, 0:4], in1=bias2[:, :, 0:4], op=ALU.add)
-        nc.scalar.activation(out=sig[:], in_=d4[:], func=ACT.Sigmoid)
-        nc.scalar.activation(out=sq[:], in_=sig[:, :, 2:4], func=ACT.Square, scale=2.0)
-        nc.scalar.activation(out=res2[:, :, 0:2], in_=sig[:, :, 0:2], func=ACT.Copy, scale=2.0, bias=-0.5)
+        for a in range(NA):
+            fields_add("l1_%d" % a, live["o", "l1", a], bias1(a, 0, 4))
+        for a in range(NA):
+            fields_scalar("l1_%d" % a, res1[:, a])
+        for a in range(NA):
+            nc.vector.tensor_tensor(out=res1[:, a, :, 4:P], in0=live["o", "l1", a][:, :, 4:P], in1=bias1(a, 4, P),
+                                    op=ALU.add)
+            nc.vector.tensor_tensor(out=res1[:, a, :, 2:4], in0=live["sq", "l1_%d" % a][:],
+                                    in1=anc[:, 6 + 2 * a:8 + 2 * a].unsqueeze(1).to_broadcast([P, 4, 2]), op=ALU.mult)
+            nc.sync.dma_start(out=out1[a], in_=res1[:, a].rearrange("p (n i) j -> p n (i j)", n=2))
+            if a == 1:
+                fields_add("l2", bank2, bias2[:, :, 0:4])
+                fields_scalar("l2", res2)
         nc.vector.tensor_tensor(out=res2[:, :, 4:P], in0=bank2[:, :, 4:P], in1=bias2[:, :, 4:P], op=ALU.add)
-        nc.vector.tensor_tensor(out=res2[:, :, 2:4], in0=sq[:],
+        nc.vector.tensor_tensor(out=res2[:, :, 2:4], in0=live["sq", "l2"][:],
                                 in1=anc[:, 12:18].rearrange("p (a j) -> p a j", j=2), op=ALU.mult)
         for n in range(2):
             nc.sync.dma_start(out=out[n, 3840:4032, :].rearrange("(a c) j -> c a j", a=NA),

@@ -36,10 +36,6 @@ def tile_head_kernel(tc, f0_bytes, f0_scale, f1, f2, w0, b0, w1, b1, w2, b2, anc
         nc.vector.memset(ones[:], 1.0)
         brow = keep.tile([P, 1184], BF16, name="brow")
         nc.vector.memset(brow[:], 0.0)
-        nc.gpsimd.dma_start(out=brow[0:1, 0:384], in_=b0.unsqueeze(0))
-        nc.gpsimd.dma_start(out=brow[0:1, 384:402], in_=anchors.rearrange("(o l) a j -> o (l a j)", o=1))
-        nc.gpsimd.dma_start(out=brow[0:1, 416:800], in_=b1.unsqueeze(0))
-        nc.gpsimd.dma_start(out=brow[0:1, 800:1184], in_=b2.unsqueeze(0))
 
         f0v = [f0_bytes[n].rearrange("(p t) h w -> p t (h w)", t=4) for n in range(2)]
         f0b_00 = keep.tile([P, 4, 512], U8, name="f0b_00")
@@ -50,19 +46,23 @@ def tile_head_kernel(tc, f0_bytes, f0_scale, f1, f2, w0, b0, w1, b1, w2, b2, anc
         nc.sync.dma_start(out=w0sb[:], in_=w0.rearrange("(a p) k -> p a k", p=P))
         f0b_01 = keep.tile([P, 4, 512], U8, name="f0b_01")
         nc.sync.dma_start(out=f0b_01[:], in_=f0v[0][:, :, 512:1024])
+        nc.sync.dma_start(out=brow[0:1, 0:384], in_=b0.unsqueeze(0))
+        nc.sync.dma_start(out=brow[0:1, 384:402], in_=anchors.rearrange("(o l) a j -> o (l a j)", o=1))
         f0b_1 = keep.tile([P, 4, 1024], U8, name="f0b_1")
         nc.sync.dma_start(out=f0b_1[:], in_=f0v[1])
+        w1sb = keep.tile([P, NA, 512], BF16, name="w1sb")
+        nc.sync.dma_start(out=w1sb[:], in_=w1.rearrange("(a p) k -> p a k", p=P))
         f1sb = keep.tile([P, 2, 4, 256], BF16, name="f1sb")
         nc.sync.dma_start(out=f1sb[:].rearrange("p n t c -> p n (t c)"),
                           in_=f1.rearrange("n (p t) h w -> p n (t h w)", t=4))
-        w1sb = keep.tile([P, NA, 512], BF16, name="w1sb")
-        nc.sync.dma_start(out=w1sb[:], in_=w1.rearrange("(a p) k -> p a k", p=P))
         w2sb = keep.tile([P, NA, 1024], BF16, name="w2sb")
         nc.sync.dma_start(out=w2sb[:], in_=w2.rearrange("(a p) k -> p a k", p=P))
         f2sb = keep.tile([P, 2, 2, 4, 64], BF16, name="f2sb")
         for n in range(2):
             nc.sync.dma_start(out=f2sb[:, n].rearrange("p g t c -> p g (t c)"),
                               in_=f2[n].rearrange("(g p t) h w -> p g (t h w)", g=2, t=4))
+        nc.sync.dma_start(out=brow[0:1, 416:800], in_=b1.unsqueeze(0))
+        nc.sync.dma_start(out=brow[0:1, 800:1184], in_=b2.unsqueeze(0))
         byte_src = [f0b_00[:], f0b_01[:], f0b_1[:, :, 0:512], f0b_1[:, :, 512:1024]]
 
         bias = keep.tile([P, 1152], BF16, name="bias")
@@ -76,13 +76,10 @@ def tile_head_kernel(tc, f0_bytes, f0_scale, f1, f2, w0, b0, w1, b1, w2, b2, anc
 
         wq = [mx_tiles(1536, "w0"), mx_tiles(1536, "w1"), mx_tiles(3072, "w2")]
         wsb = [w0sb, w1sb, w2sb]
-        wide = [keep.tile([P, 4, 512], BF16, name="wide%d" % k, tag=("ovA" if k == 1 else "wide%d" % k),
-                          align_bytes=64) for k in range(4)]
+        wide = [keep.tile([P, 4, 512], BF16, name="wide%d" % k) for k in range(4)]
         f0q = [mx_tiles(2048, "f0_%d" % k) for k in range(4)]
-        f1c = keep.tile([P, 512], U32, name="c_f1", align_bytes=64)
-        f1s = keep.tile([P, 512], U8, name="s_f1", align_bytes=64)
-        f2c = keep.tile([P, 256], U32, name="c_f2", align_bytes=64)
-        f2s = keep.tile([P, 256], U8, name="s_f2", align_bytes=64)
+        f1q = mx_tiles(2048, "f1")
+        f2q = mx_tiles(1024, "f2")
         res0 = [keep.tile([P, NA, 4, P], F32, name="res0_%d" % k) for k in range(4)]
         res1 = keep.tile([P, NA, 4, P], F32, name="res1")
         res2 = keep.tile([P, NA, P], F32, name="res2")
@@ -165,7 +162,7 @@ def tile_head_kernel(tc, f0_bytes, f0_scale, f1, f2, w0, b0, w1, b1, w2, b2, anc
 
         def decode0_scalar(k):
             sig = keep.tile([P, NA, 4, 4], F32, name="sig0_%d" % k)
-            sq = keep.tile([P, NA, 4, 2], F32, name="sq0_%d" % k, tag=["ovB", "ovC", "sq0_2", "sq0_3"][k], align_bytes=64)
+            sq = keep.tile([P, NA, 4, 2], F32, name="sq0_%d" % k)
             nc.scalar.activation(out=sig[:], in_=res0[k][:, :, :, 0:4], func=ACT.Sigmoid)
             nc.scalar.activation(out=sq[:], in_=sig[:, :, :, 2:4], func=ACT.Square, scale=2.0)
             nc.scalar.activation(out=res0[k][:, :, :, 0:2], in_=sig[:, :, :, 0:2], func=ACT.Copy, scale=2.0, bias=-0.5)
@@ -210,18 +207,6 @@ def tile_head_kernel(tc, f0_bytes, f0_scale, f1, f2, w0, b0, w1, b1, w2, b2, anc
         bias2 = bias[:, 768:1152].rearrange("p (a j) -> p a j", a=NA)
         out1 = out[:, 3072:3840, :].rearrange("n (a p i) j -> a p n (i j)", a=NA, i=2)
 
-        def gpsimd_interleave(dst, src):
-            nc.gpsimd.tensor_scalar(out=dst, in0=src, scalar1=1.0, scalar2=0.0, op0=ALU.mult, op1=ALU.add)
-
-        def interleave1(n, tagname):
-            g = keep.tile([P, 1024], BF16, name="g_f1_%d" % n, tag=tagname, align_bytes=64)
-            gpsimd_interleave(g[:].rearrange("p (i m t) -> p i m t", i=2, t=4),
-                              f1sb[:, n].rearrange("p t (m i) -> p i m t", i=2))
-            live["g_f1", n] = g
-
-        def quantize1(n):
-            quantize((live["g_f1", n], f1c[:, n * 256:(n + 1) * 256], f1s[:, n * 256:(n + 1) * 256]), 0, 1024)
-
         widen(0, 0, "S")
         widen(0, 1, "V")
         widen(0, 2, "V")
@@ -244,77 +229,79 @@ def tile_head_kernel(tc, f0_bytes, f0_scale, f1, f2, w0, b0, w1, b1, w2, b2, anc
         for t in range(4):
             widen(2, t, "S")
         interleave0(1, "V")
-        interleave1(0, "ovA")
-        for a in range(NA):
-            add0(0, a)
+        add0(0, 0)
         quantize(f0q[1], 0, 2048)
+        add0(0, 1)
+        add0(0, 2)
         matmuls(1, f0q[1], 0)
-        w_transposes(1, 0, 2)
-        w_transposes(1, 2, 1)
-        w_transposes(2, 0, 2)
-        w_transposes(2, 2, 2)
-        w_transposes(2, 4, 2)
-        for t in range(3):
+        for t in range(4):
             widen(3, t, "S")
         decode0_scalar(0)
-        widen(3, 3, "S")
         interleave0(2, "V")
         decode0_vector(0)
         store0(0)
-        interleave1(1, "ovB")
-        for a in range(NA):
-            add0(1, a)
+        add0(1, 0)
         quantize(f0q[2], 0, 2048)
+        add0(1, 1)
+        add0(1, 2)
+        w_transposes(1, 0, 2)
+        w_transposes(1, 2, 1)
         matmuls(2, f0q[2], 0)
         interleave0(3, "S")
         decode0_scalar(1)
-        quantize1(0)
-        quantize1(1)
-        decode0_vector(1)
-        store0(1)
-        f2g = keep.tile([P, 1024], BF16, name="g_f2", tag="ovC", align_bytes=64)
-        for g in range(2):
-            gpsimd_interleave(f2g[:, g * 512:(g + 1) * 512].rearrange("p (n c t) -> p n c t", n=2, t=4),
-                              f2sb[:, :, g].rearrange("p n t c -> p n c t"))
-        for a in range(NA):
-            add0(2, a)
+        add0(2, 0)
         quantize(f0q[3], 0, 2048)
+        add0(2, 1)
+        add0(2, 2)
         w_empty(1, 0, 2)
         w_empty(1, 2, 1)
+        decode0_vector(1)
+        store0(1)
+        matmuls(3, f0q[3], 0)
+        w_transposes(2, 0, 2)
+        w_transposes(2, 2, 2)
+        w_transposes(2, 4, 2)
+        bias12_matmul()
+        quantize(wq[1], 0, 1024)
+        quantize(wq[1], 1024, 512)
+        for n in range(2):
+            nc.scalar.copy(out=f1q[0][:, n * 1024:(n + 1) * 1024].rearrange("p (i m t) -> p i m t", i=2, t=4),
+                           in_=f1sb[:, n].rearrange("p t (m i) -> p i m t", i=2))
+        add0(3, 0)
+        decode0_scalar(2)
+        quantize(f1q, 0, 2048)
+        add0(3, 1)
+        add0(3, 2)
+        decode0_vector(2)
+        store0(2)
+        matmuls("l1", f1q, 1)
         w_empty(2, 0, 2)
         w_empty(2, 2, 2)
         w_empty(2, 4, 2)
-        bias12_matmul()
-        matmuls(3, f0q[3], 0)
-        decode0_scalar(2)
-        quantize(wq[1], 0, 1024)
-        quantize(wq[1], 1024, 512)
-        decode0_vector(2)
-        store0(2)
-        for a in range(NA):
-            add0(3, a)
-        matmuls("l1", (None, f1c, f1s), 1)
-        bias12_empty()
-        decode0_scalar(3)
         quantize(wq[2], 0, 2048)
+        decode0_scalar(3)
+        bias12_empty()
+        for g in range(2):
+            nc.scalar.copy(out=f2q[0][:, g * 512:(g + 1) * 512].rearrange("p (n c t) -> p n c t", n=2, t=4),
+                           in_=f2sb[:, :, g].rearrange("p n t c -> p n c t"))
+        quantize(wq[2], 2048, 1024)
         decode0_vector(3)
         store0(3)
-        quantize(wq[2], 2048, 1024)
-        quantize((f2g, f2c, f2s), 0, 1024)
+        for a in range(NA):
+            fields_add("l1_%d" % a, live["o", "l1", a], bias1(a, 0, 4))
+        for a in range(NA):
+            fields_scalar("l1_%d" % a, res1[:, a])
+        quantize(f2q, 0, 1024)
         bank2 = psum.tile([P, NA, P], F32, tag="bank", name="o_l2")
         for a in range(NA):
             for g in range(2):
                 q = g * NA + a
                 nc.tensor.matmul_mx(out=bank2[:, a, :],
-                                    lhsT=f2c[:, g * P:(g + 1) * P].bitcast(FP8X4),
-                                    lhsT_scale=f2s[:, g * P:(g + 1) * P],
+                                    lhsT=f2q[1][:, g * P:(g + 1) * P].bitcast(FP8X4),
+                                    lhsT_scale=f2q[2][:, g * P:(g + 1) * P],
                                     rhs=wq[2][1][:, q * P:(q + 1) * P].bitcast(FP8X4),
                                     rhs_scale=wq[2][2][:, q * P:(q + 1) * P],
                                     start=(g == 0), stop=(g == 1))
-        for a in range(NA):
-            fields_add("l1_%d" % a, live["o", "l1", a], bias1(a, 0, 4))
-        for a in range(NA):
-            fields_scalar("l1_%d" % a, res1[:, a])
         for a in range(NA):
             nc.vector.tensor_tensor(out=res1[:, a, :, 4:P], in0=live["o", "l1", a][:, :, 4:P], in1=bias1(a, 4, P),
                                     op=ALU.add)

@@ -16,7 +16,7 @@ P = 128
 NA = 3
 FLOPS = 2 * 384 * (512 * 2048 + 512 * 512 + 1024 * 128)
 
-PERM = [False, False, False, True]
+PERM = [False, False, False, False]
 
 
 def tile_head_kernel(tc, f0_bytes, f0_scale, f1, f2, w0, b0, w1, b1, w2, b2, anchors, out):
@@ -38,18 +38,19 @@ def tile_head_kernel(tc, f0_bytes, f0_scale, f1, f2, w0, b0, w1, b1, w2, b2, anc
         nc.vector.memset(brow[:], 0.0)
 
         f0v = [f0_bytes[n].rearrange("(p t) h w -> p t (h w)", t=4) for n in range(2)]
-        f0b_00 = keep.tile([P, 4, 512], U8, name="f0b_00")
-        nc.sync.dma_start(out=f0b_00[:], in_=f0v[0][:, :, 0:512])
         sc = keep.tile([P, 4], F32, name="sc")
         nc.sync.dma_start(out=sc[:], in_=f0_scale[0, :, 0, 0].rearrange("(p t) -> p t", t=4))
+        f0b_00 = [keep.tile([P, 512], U8, name="f0b_00_%d" % t) for t in range(4)]
+        for t in range(4):
+            nc.sync.dma_start(out=f0b_00[t][:], in_=f0v[0][:, t, 0:512])
         w0sb = keep.tile([P, NA, 512], BF16, name="w0sb")
         nc.sync.dma_start(out=w0sb[:], in_=w0.rearrange("(a p) k -> p a k", p=P))
         f0b_01 = keep.tile([P, 4, 512], U8, name="f0b_01")
         nc.sync.dma_start(out=f0b_01[:], in_=f0v[0][:, :, 512:1024])
-        nc.sync.dma_start(out=brow[0:1, 0:384], in_=b0.unsqueeze(0))
-        nc.sync.dma_start(out=brow[0:1, 384:402], in_=anchors.rearrange("(o l) a j -> o (l a j)", o=1))
         f0b_1 = keep.tile([P, 4, 1024], U8, name="f0b_1")
         nc.sync.dma_start(out=f0b_1[:], in_=f0v[1])
+        nc.sync.dma_start(out=brow[0:1, 0:384], in_=b0.unsqueeze(0))
+        nc.sync.dma_start(out=brow[0:1, 384:402], in_=anchors.rearrange("(o l) a j -> o (l a j)", o=1))
         w1sb = keep.tile([P, NA, 512], BF16, name="w1sb")
         nc.sync.dma_start(out=w1sb[:], in_=w1.rearrange("(a p) k -> p a k", p=P))
         f1sb = keep.tile([P, 2, 4, 256], BF16, name="f1sb")
@@ -63,7 +64,10 @@ def tile_head_kernel(tc, f0_bytes, f0_scale, f1, f2, w0, b0, w1, b1, w2, b2, anc
                               in_=f2[n].rearrange("(g p t) h w -> p g (t h w)", g=2, t=4))
         nc.sync.dma_start(out=brow[0:1, 416:800], in_=b1.unsqueeze(0))
         nc.sync.dma_start(out=brow[0:1, 800:1184], in_=b2.unsqueeze(0))
-        byte_src = [f0b_00[:], f0b_01[:], f0b_1[:, :, 0:512], f0b_1[:, :, 512:1024]]
+        byte_src = [[f0b_00[t][:] for t in range(4)],
+                    [f0b_01[:, t, :] for t in range(4)],
+                    [f0b_1[:, t, 0:512] for t in range(4)],
+                    [f0b_1[:, t, 512:1024] for t in range(4)]]
 
         bias = keep.tile([P, 1152], BF16, name="bias")
         anc = keep.tile([P, 18], F32, name="anc")
@@ -86,7 +90,7 @@ def tile_head_kernel(tc, f0_bytes, f0_scale, f1, f2, w0, b0, w1, b1, w2, b2, anc
         live = {}
 
         def widen(k, t, eng):
-            src = byte_src[k][:, t, :].bitcast(FP8)
+            src = byte_src[k][t].bitcast(FP8)
             if eng == "S":
                 nc.scalar.activation(out=wide[k][:, t, :], in_=src, func=ACT.Copy, scale=sc[:, t:t + 1])
             else:
@@ -98,12 +102,20 @@ def tile_head_kernel(tc, f0_bytes, f0_scale, f1, f2, w0, b0, w1, b1, w2, b2, anc
                 dst = f0q[k][0][:].rearrange("p (i m t) -> p i m t", i=4, t=4)
                 src = wide[k][:].rearrange("p t (m i) -> p i m t", i=4)
             else:
-                dst = f0q[k][0][:].rearrange("p (c t) -> p c t", t=4)
-                src = wide[k][:].rearrange("p t c -> p c t")
+                dst = f0q[k][0][:].rearrange("p (c i t) -> p c t i", i=4, t=4)
+                src = wide[k][:].rearrange("p t (c i) -> p c t i", i=4)
             if eng == "V":
                 nc.vector.tensor_copy(out=dst, in_=src)
             else:
                 nc.scalar.copy(out=dst, in_=src)
+
+        def interleave1(n):
+            nc.scalar.copy(out=f1q[0][:, n * 1024:(n + 1) * 1024].rearrange("p (i m t) -> p i m t", i=2, t=4),
+                           in_=f1sb[:, n].rearrange("p t (m i) -> p i m t", i=2))
+
+        def interleave2(g):
+            nc.vector.tensor_copy(out=f2q[0][:, g * 512:(g + 1) * 512].rearrange("p (n c t) -> p n c t", n=2, t=4),
+                                  in_=f2sb[:, :, g].rearrange("p n t c -> p n c t"))
 
         def quantize(q3, c0, wd):
             nc.vector.quantize_mx(out=q3[1][:, c0 // 4:(c0 + wd) // 4].bitcast(FP8X4),
@@ -251,12 +263,12 @@ def tile_head_kernel(tc, f0_bytes, f0_scale, f1, f2, w0, b0, w1, b1, w2, b2, anc
         decode0_scalar(1)
         add0(2, 0)
         quantize(f0q[3], 0, 2048)
+        decode0_vector(1)
+        store0(1)
         add0(2, 1)
         add0(2, 2)
         w_empty(1, 0, 2)
         w_empty(1, 2, 1)
-        decode0_vector(1)
-        store0(1)
         matmuls(3, f0q[3], 0)
         w_transposes(2, 0, 2)
         w_transposes(2, 2, 2)
@@ -264,16 +276,15 @@ def tile_head_kernel(tc, f0_bytes, f0_scale, f1, f2, w0, b0, w1, b1, w2, b2, anc
         bias12_matmul()
         quantize(wq[1], 0, 1024)
         quantize(wq[1], 1024, 512)
-        for n in range(2):
-            nc.scalar.copy(out=f1q[0][:, n * 1024:(n + 1) * 1024].rearrange("p (i m t) -> p i m t", i=2, t=4),
-                           in_=f1sb[:, n].rearrange("p t (m i) -> p i m t", i=2))
-        add0(3, 0)
+        interleave1(0)
         decode0_scalar(2)
-        quantize(f1q, 0, 2048)
-        add0(3, 1)
-        add0(3, 2)
+        interleave1(1)
+        add0(3, 0)
         decode0_vector(2)
         store0(2)
+        add0(3, 1)
+        quantize(f1q, 0, 2048)
+        add0(3, 2)
         matmuls("l1", f1q, 1)
         w_empty(2, 0, 2)
         w_empty(2, 2, 2)
@@ -281,12 +292,11 @@ def tile_head_kernel(tc, f0_bytes, f0_scale, f1, f2, w0, b0, w1, b1, w2, b2, anc
         quantize(wq[2], 0, 2048)
         decode0_scalar(3)
         bias12_empty()
-        for g in range(2):
-            nc.scalar.copy(out=f2q[0][:, g * 512:(g + 1) * 512].rearrange("p (n c t) -> p n c t", n=2, t=4),
-                           in_=f2sb[:, :, g].rearrange("p n t c -> p n c t"))
-        quantize(wq[2], 2048, 1024)
+        interleave2(0)
         decode0_vector(3)
         store0(3)
+        interleave2(1)
+        quantize(wq[2], 2048, 1024)
         for a in range(NA):
             fields_add("l1_%d" % a, live["o", "l1", a], bias1(a, 0, 4))
         for a in range(NA):

@@ -72,8 +72,8 @@ def tile_head_kernel(tc, f0_bytes, f0_scale, f1, f2, w0, b0, w1, b1, w2, b2, anc
         bias = keep.tile([P, 1152], BF16, name="bias")
         anc = keep.tile([P, 18], F32, name="anc")
 
-        def mx_tiles(width, tagname):
-            grouped = keep.tile([P, width], BF16, name="g_" + tagname, align_bytes=64)
+        def mx_tiles(width, tagname, gtag=None):
+            grouped = keep.tile([P, width], BF16, name="g_" + tagname, tag=(gtag or "g_" + tagname), align_bytes=64)
             codes = keep.tile([P, width // 4], U32, name="c_" + tagname, align_bytes=64)
             scales = keep.tile([P, width // 4], U8, name="s_" + tagname, align_bytes=64)
             return grouped, codes, scales
@@ -81,8 +81,9 @@ def tile_head_kernel(tc, f0_bytes, f0_scale, f1, f2, w0, b0, w1, b1, w2, b2, anc
         wq = [mx_tiles(1536, "w0"), mx_tiles(1536, "w1"), mx_tiles(3072, "w2")]
         wsb = [w0sb, w1sb, w2sb]
         wide = [keep.tile([P, 4, 512], BF16, name="wide%d" % k) for k in range(4)]
-        f0q = [mx_tiles(2048, "f0_%d" % k) for k in range(4)]
-        f1q = mx_tiles(2048, "f1")
+        f0q = [mx_tiles(2048, "f0_%d" % k, [None, "ovA", "ovB", None][k]) for k in range(4)]
+        f1c = keep.tile([P, 512], U32, name="c_f1", align_bytes=64)
+        f1s = keep.tile([P, 512], U8, name="s_f1", align_bytes=64)
         f2q = mx_tiles(1024, "f2")
         res0 = [keep.tile([P, NA, 4, P], F32, name="res0_%d" % k) for k in range(4)]
         res1 = keep.tile([P, NA, 4, P], F32, name="res1")
@@ -109,13 +110,24 @@ def tile_head_kernel(tc, f0_bytes, f0_scale, f1, f2, w0, b0, w1, b1, w2, b2, anc
             else:
                 nc.scalar.copy(out=dst, in_=src)
 
-        def interleave1(n):
-            nc.scalar.copy(out=f1q[0][:, n * 1024:(n + 1) * 1024].rearrange("p (i m t) -> p i m t", i=2, t=4),
-                           in_=f1sb[:, n].rearrange("p t (m i) -> p i m t", i=2))
+        def interleave1(piece, eng, tagname):
+            n, i = divmod(piece, 2)
+            g = keep.tile([P, 512], BF16, name="g_f1_%d" % piece, tag=tagname, align_bytes=64)
+            dst = g[:].rearrange("p (m t) -> p m t", t=4)
+            src = f1sb[:, n].rearrange("p t (m i) -> p i m t", i=2)[:, i]
+            if eng == "G":
+                nc.gpsimd.tensor_scalar(out=dst, in0=src, scalar1=1.0, scalar2=0.0, op0=ALU.mult, op1=ALU.add)
+            else:
+                nc.scalar.copy(out=dst, in_=src)
+            live["g_f1", piece] = g
+
+        def quantize1(piece):
+            cols = slice(piece * P, (piece + 1) * P)
+            quantize((live["g_f1", piece], f1c[:, cols], f1s[:, cols]), 0, 512)
 
         def interleave2(g):
-            nc.vector.tensor_copy(out=f2q[0][:, g * 512:(g + 1) * 512].rearrange("p (n c t) -> p n c t", n=2, t=4),
-                                  in_=f2sb[:, :, g].rearrange("p n t c -> p n c t"))
+            nc.scalar.copy(out=f2q[0][:, g * 512:(g + 1) * 512].rearrange("p (n c t) -> p n c t", n=2, t=4),
+                           in_=f2sb[:, :, g].rearrange("p n t c -> p n c t"))
 
         def quantize(q3, c0, wd):
             nc.vector.quantize_mx(out=q3[1][:, c0 // 4:(c0 + wd) // 4].bitcast(FP8X4),
@@ -174,7 +186,7 @@ def tile_head_kernel(tc, f0_bytes, f0_scale, f1, f2, w0, b0, w1, b1, w2, b2, anc
 
         def decode0_scalar(k):
             sig = keep.tile([P, NA, 4, 4], F32, name="sig0_%d" % k)
-            sq = keep.tile([P, NA, 4, 2], F32, name="sq0_%d" % k)
+            sq = keep.tile([P, NA, 4, 2], F32, name="sq0_%d" % k, tag=("ovC" if k == 1 else "sq0_%d" % k), align_bytes=64)
             nc.scalar.activation(out=sig[:], in_=res0[k][:, :, :, 0:4], func=ACT.Sigmoid)
             nc.scalar.activation(out=sq[:], in_=sig[:, :, :, 2:4], func=ACT.Square, scale=2.0)
             nc.scalar.activation(out=res0[k][:, :, :, 0:2], in_=sig[:, :, :, 0:2], func=ACT.Copy, scale=2.0, bias=-0.5)
@@ -243,6 +255,7 @@ def tile_head_kernel(tc, f0_bytes, f0_scale, f1, f2, w0, b0, w1, b1, w2, b2, anc
         interleave0(1, "V")
         add0(0, 0)
         quantize(f0q[1], 0, 2048)
+        interleave1(0, "G", "ovA")
         add0(0, 1)
         add0(0, 2)
         matmuls(1, f0q[1], 0)
@@ -254,6 +267,7 @@ def tile_head_kernel(tc, f0_bytes, f0_scale, f1, f2, w0, b0, w1, b1, w2, b2, anc
         store0(0)
         add0(1, 0)
         quantize(f0q[2], 0, 2048)
+        interleave1(1, "G", "ovB")
         add0(1, 1)
         add0(1, 2)
         w_transposes(1, 0, 2)
@@ -265,37 +279,38 @@ def tile_head_kernel(tc, f0_bytes, f0_scale, f1, f2, w0, b0, w1, b1, w2, b2, anc
         quantize(f0q[3], 0, 2048)
         decode0_vector(1)
         store0(1)
+        interleave1(2, "G", "ovC")
         add0(2, 1)
         add0(2, 2)
         w_empty(1, 0, 2)
         w_empty(1, 2, 1)
         matmuls(3, f0q[3], 0)
+        bias12_matmul()
         w_transposes(2, 0, 2)
         w_transposes(2, 2, 2)
         w_transposes(2, 4, 2)
-        bias12_matmul()
         quantize(wq[1], 0, 1024)
         quantize(wq[1], 1024, 512)
-        interleave1(0)
+        interleave1(3, "S", "g_f1_3")
+        interleave2(0)
         decode0_scalar(2)
-        interleave1(1)
+        bias12_empty()
         add0(3, 0)
         decode0_vector(2)
         store0(2)
         add0(3, 1)
-        quantize(f1q, 0, 2048)
+        for piece in range(4):
+            quantize1(piece)
         add0(3, 2)
-        matmuls("l1", f1q, 1)
+        matmuls("l1", (None, f1c, f1s), 1)
         w_empty(2, 0, 2)
         w_empty(2, 2, 2)
         w_empty(2, 4, 2)
         quantize(wq[2], 0, 2048)
         decode0_scalar(3)
-        bias12_empty()
-        interleave2(0)
+        interleave2(1)
         decode0_vector(3)
         store0(3)
-        interleave2(1)
         quantize(wq[2], 2048, 1024)
         for a in range(NA):
             fields_add("l1_%d" % a, live["o", "l1", a], bias1(a, 0, 4))

@@ -81,7 +81,7 @@ def tile_head_kernel(tc, f0_bytes, f0_scale, f1, f2, w0, b0, w1, b1, w2, b2, anc
         wq = [mx_tiles(1536, "w0"), mx_tiles(1536, "w1"), mx_tiles(3072, "w2")]
         wsb = [w0sb, w1sb, w2sb]
         wide = [keep.tile([P, 4, 512], BF16, name="wide%d" % k) for k in range(4)]
-        f0q = [mx_tiles(2048, "f0_%d" % k, [None, "ovA", "ovB", None][k]) for k in range(4)]
+        f0q = [mx_tiles(2048, "f0_%d" % k, [None, "ovA", None, None][k]) for k in range(4)]
         f1c = keep.tile([P, 512], U32, name="c_f1", align_bytes=64)
         f1s = keep.tile([P, 512], U8, name="s_f1", align_bytes=64)
         f2q = mx_tiles(1024, "f2")
@@ -98,17 +98,29 @@ def tile_head_kernel(tc, f0_bytes, f0_scale, f1, f2, w0, b0, w1, b1, w2, b2, anc
                 nc.vector.tensor_scalar(out=wide[k][:, t, :], in0=src, scalar1=sc[:, t:t + 1], scalar2=None,
                                         op0=ALU.mult)
 
-        def interleave0(k, eng):
-            if PERM[k]:
-                dst = f0q[k][0][:].rearrange("p (i m t) -> p i m t", i=4, t=4)
-                src = wide[k][:].rearrange("p t (m i) -> p i m t", i=4)
+        def interleave0(k, eng, c0=0, c1=512, tagname=None):
+            if tagname is None:
+                g = f0q[k][0][:, 4 * c0:4 * c1]
             else:
-                dst = f0q[k][0][:].rearrange("p (c i t) -> p c t i", i=4, t=4)
-                src = wide[k][:].rearrange("p t (c i) -> p c t i", i=4)
+                gt = keep.tile([P, 4 * (c1 - c0)], BF16, name="gG_%d" % k, tag=tagname, align_bytes=64)
+                live["gG", k] = gt
+                g = gt[:]
+            if eng == "G":
+                nc.gpsimd.tensor_scalar(out=g.rearrange("p (m t) -> p m t", t=4),
+                                        in0=wide[k][:, :, c0:c1].rearrange("p t m -> p m t"),
+                                        scalar1=1.0, scalar2=0.0, op0=ALU.mult, op1=ALU.add)
+                return
+            dst = g.rearrange("p (c i t) -> p c t i", i=4, t=4)
+            src = wide[k][:, :, c0:c1].rearrange("p t (c i) -> p c t i", i=4)
             if eng == "V":
                 nc.vector.tensor_copy(out=dst, in_=src)
             else:
                 nc.scalar.copy(out=dst, in_=src)
+
+        def quantize_half(k, half):
+            src = f0q[k][0][:, 0:1024] if half == 0 else live["gG", k][:]
+            nc.vector.quantize_mx(out=f0q[k][1][:, half * 256:(half + 1) * 256].bitcast(FP8X4),
+                                  scales=f0q[k][2][:, half * 256:(half + 1) * 256], in_=src)
 
         def interleave1(piece, eng, tagname):
             n, i = divmod(piece, 2)
@@ -125,9 +137,16 @@ def tile_head_kernel(tc, f0_bytes, f0_scale, f1, f2, w0, b0, w1, b1, w2, b2, anc
             cols = slice(piece * P, (piece + 1) * P)
             quantize((live["g_f1", piece], f1c[:, cols], f1s[:, cols]), 0, 512)
 
-        def interleave2(g):
-            nc.scalar.copy(out=f2q[0][:, g * 512:(g + 1) * 512].rearrange("p (n c t) -> p n c t", n=2, t=4),
-                           in_=f2sb[:, :, g].rearrange("p n t c -> p n c t"))
+        def interleave2(g, eng):
+            if eng == "S":
+                nc.scalar.copy(out=f2q[0][:, g * 512:(g + 1) * 512].rearrange("p (n c t) -> p n c t", n=2, t=4),
+                               in_=f2sb[:, :, g].rearrange("p n t c -> p n c t"))
+            else:
+                for n in range(2):
+                    nc.gpsimd.tensor_scalar(
+                        out=f2q[0][:, g * 512 + n * 256:g * 512 + (n + 1) * 256].rearrange("p (c t) -> p c t", t=4),
+                        in0=f2sb[:, n, g].rearrange("p t c -> p c t"),
+                        scalar1=1.0, scalar2=0.0, op0=ALU.mult, op1=ALU.add)
 
         def quantize(q3, c0, wd):
             nc.vector.quantize_mx(out=q3[1][:, c0 // 4:(c0 + wd) // 4].bitcast(FP8X4),
@@ -186,14 +205,14 @@ def tile_head_kernel(tc, f0_bytes, f0_scale, f1, f2, w0, b0, w1, b1, w2, b2, anc
 
         def decode0_scalar(k):
             sig = keep.tile([P, NA, 4, 4], F32, name="sig0_%d" % k)
-            sq = keep.tile([P, NA, 4, 2], F32, name="sq0_%d" % k, tag=("ovC" if k == 1 else "sq0_%d" % k), align_bytes=64)
+            sq = keep.tile([P, NA, 4, 2], F32, name="sq0_%d" % k, tag=("ovC" if k == 2 else "sq0_%d" % k), align_bytes=64)
             nc.scalar.activation(out=sig[:], in_=res0[k][:, :, :, 0:4], func=ACT.Sigmoid)
             nc.scalar.activation(out=sq[:], in_=sig[:, :, :, 2:4], func=ACT.Square, scale=2.0)
             nc.scalar.activation(out=res0[k][:, :, :, 0:2], in_=sig[:, :, :, 0:2], func=ACT.Copy, scale=2.0, bias=-0.5)
             live["sq", k] = sq
 
-        def decode0_vector(k):
-            nc.vector.tensor_tensor(
+        def decode0_vector(k, eng="V"):
+            (nc.vector if eng == "V" else nc.gpsimd).tensor_tensor(
                 out=res0[k][:, :, :, 2:4], in0=live["sq", k][:],
                 in1=anc[:, 0:6].rearrange("p (a j) -> p a j", j=2).unsqueeze(2).to_broadcast([P, NA, 4, 2]),
                 op=ALU.mult)
@@ -255,60 +274,64 @@ def tile_head_kernel(tc, f0_bytes, f0_scale, f1, f2, w0, b0, w1, b1, w2, b2, anc
         interleave0(1, "V")
         add0(0, 0)
         quantize(f0q[1], 0, 2048)
-        interleave1(0, "G", "ovA")
+        matmuls(1, f0q[1], 0)
+        interleave0(2, "S", 0, 256)
+        interleave0(2, "G", 256, 512, "ovA")
         add0(0, 1)
         add0(0, 2)
-        matmuls(1, f0q[1], 0)
-        for t in range(4):
-            widen(3, t, "S")
         decode0_scalar(0)
-        interleave0(2, "V")
+        add0(1, 0)
         decode0_vector(0)
         store0(0)
-        add0(1, 0)
-        quantize(f0q[2], 0, 2048)
-        interleave1(1, "G", "ovB")
-        add0(1, 1)
-        add0(1, 2)
+        quantize_half(2, 0)
+        quantize_half(2, 1)
         w_transposes(1, 0, 2)
         w_transposes(1, 2, 1)
         matmuls(2, f0q[2], 0)
-        interleave0(3, "S")
+        for t in range(4):
+            widen(3, t, "S")
+        interleave1(0, "G", "ovA")
+        interleave1(1, "G", "g_f1_1")
+        add0(1, 1)
+        add0(1, 2)
         decode0_scalar(1)
-        add0(2, 0)
-        quantize(f0q[3], 0, 2048)
-        decode0_vector(1)
+        decode0_vector(1, "G")
         store0(1)
-        interleave1(2, "G", "ovC")
-        add0(2, 1)
-        add0(2, 2)
-        w_empty(1, 0, 2)
-        w_empty(1, 2, 1)
-        matmuls(3, f0q[3], 0)
-        bias12_matmul()
+        interleave0(3, "S", 0, 256)
+        interleave0(3, "G", 256, 512, "gG_3")
         w_transposes(2, 0, 2)
         w_transposes(2, 2, 2)
         w_transposes(2, 4, 2)
+        add0(2, 0)
+        add0(2, 1)
+        add0(2, 2)
+        decode0_scalar(2)
+        w_empty(1, 0, 2)
+        w_empty(1, 2, 1)
+        quantize_half(3, 0)
+        quantize_half(3, 1)
+        matmuls(3, f0q[3], 0)
         quantize(wq[1], 0, 1024)
         quantize(wq[1], 1024, 512)
-        interleave1(3, "S", "g_f1_3")
-        interleave2(0)
-        decode0_scalar(2)
-        bias12_empty()
-        add0(3, 0)
         decode0_vector(2)
         store0(2)
-        add0(3, 1)
-        for piece in range(4):
-            quantize1(piece)
-        add0(3, 2)
-        matmuls("l1", (None, f1c, f1s), 1)
+        bias12_matmul()
+        interleave1(2, "G", "ovC")
+        interleave2(0, "G")
+        interleave1(3, "S", "g_f1_3")
         w_empty(2, 0, 2)
         w_empty(2, 2, 2)
         w_empty(2, 4, 2)
-        quantize(wq[2], 0, 2048)
+        add0(3, 0)
+        add0(3, 1)
+        add0(3, 2)
         decode0_scalar(3)
-        interleave2(1)
+        for piece in range(4):
+            quantize1(piece)
+        matmuls("l1", (None, f1c, f1s), 1)
+        bias12_empty()
+        quantize(wq[2], 0, 2048)
+        interleave2(1, "S")
         decode0_vector(3)
         store0(3)
         quantize(wq[2], 2048, 1024)

@@ -43,10 +43,10 @@ def tile_head_kernel(tc, f0_bytes, f0_scale, f1, f2, w0, b0, w1, b1, w2, b2, anc
         f0b_00 = [keep.tile([P, 512], U8, name="f0b_00_%d" % t) for t in range(4)]
         for t in range(4):
             nc.sync.dma_start(out=f0b_00[t][:], in_=f0v[0][:, t, 0:512])
-        w0sb = keep.tile([P, NA, 512], BF16, name="w0sb")
-        nc.sync.dma_start(out=w0sb[:], in_=w0.rearrange("(a p) k -> p a k", p=P))
         f0b_01 = keep.tile([P, 4, 512], U8, name="f0b_01")
         nc.sync.dma_start(out=f0b_01[:], in_=f0v[0][:, :, 512:1024])
+        w0sb = keep.tile([P, NA, 512], BF16, name="w0sb")
+        nc.sync.dma_start(out=w0sb[:], in_=w0.rearrange("(a p) k -> p a k", p=P))
         f0b_1 = keep.tile([P, 4, 1024], U8, name="f0b_1")
         nc.sync.dma_start(out=f0b_1[:], in_=f0v[1])
         nc.sync.dma_start(out=brow[0:1, 0:384], in_=b0.unsqueeze(0))
@@ -141,6 +141,9 @@ def tile_head_kernel(tc, f0_bytes, f0_scale, f1, f2, w0, b0, w1, b1, w2, b2, anc
             if eng == "S":
                 nc.scalar.copy(out=f2q[0][:, g * 512:(g + 1) * 512].rearrange("p (n c t) -> p n c t", n=2, t=4),
                                in_=f2sb[:, :, g].rearrange("p n t c -> p n c t"))
+            elif eng == "V":
+                nc.vector.tensor_copy(out=f2q[0][:, g * 512:(g + 1) * 512].rearrange("p (n c t) -> p n c t", n=2, t=4),
+                                      in_=f2sb[:, :, g].rearrange("p n t c -> p n c t"))
             else:
                 for n in range(2):
                     nc.gpsimd.tensor_scalar(
@@ -203,10 +206,14 @@ def tile_head_kernel(tc, f0_bytes, f0_scale, f1, f2, w0, b0, w1, b1, w2, b2, anc
             nc.vector.tensor_tensor(out=res0[k][:, a], in0=live["o", k, a][:],
                                     in1=bias[:, a * P:(a + 1) * P].unsqueeze(1).to_broadcast([P, 4, P]), op=ALU.add)
 
-        def decode0_scalar(k):
+        def decode0_sigmoid(k):
             sig = keep.tile([P, NA, 4, 4], F32, name="sig0_%d" % k)
-            sq = keep.tile([P, NA, 4, 2], F32, name="sq0_%d" % k, tag=("ovC" if k == 2 else "sq0_%d" % k), align_bytes=64)
             nc.scalar.activation(out=sig[:], in_=res0[k][:, :, :, 0:4], func=ACT.Sigmoid)
+            live["sig", k] = sig
+
+        def decode0_scalar(k):
+            sig = live["sig", k]
+            sq = keep.tile([P, NA, 4, 2], F32, name="sq0_%d" % k, tag=("ovC" if k == 2 else "sq0_%d" % k), align_bytes=64)
             nc.scalar.activation(out=sq[:], in_=sig[:, :, :, 2:4], func=ACT.Square, scale=2.0)
             nc.scalar.activation(out=res0[k][:, :, :, 0:2], in_=sig[:, :, :, 0:2], func=ACT.Copy, scale=2.0, bias=-0.5)
             live["sq", k] = sq
@@ -234,12 +241,15 @@ def tile_head_kernel(tc, f0_bytes, f0_scale, f1, f2, w0, b0, w1, b1, w2, b2, anc
             nc.vector.tensor_tensor(out=d4[:], in0=bank[:, :, 0:4], in1=bias_ap, op=ALU.add)
             live["d4", tagname] = d4
 
-        def fields_scalar(tagname, res_ap):
+        def fields_sigmoid(tagname):
             d4 = live["d4", tagname]
-            reps = d4.shape[1]
-            sig = keep.tile([P, reps, 4], F32, name="sg_" + tagname)
-            sq = keep.tile([P, reps, 2], F32, name="sq_" + tagname)
+            sig = keep.tile([P, d4.shape[1], 4], F32, name="sg_" + tagname)
             nc.scalar.activation(out=sig[:], in_=d4[:], func=ACT.Sigmoid)
+            live["sg", tagname] = sig
+
+        def fields_scalar(tagname, res_ap):
+            sig = live["sg", tagname]
+            sq = keep.tile([P, sig.shape[1], 2], F32, name="sq_" + tagname)
             nc.scalar.activation(out=sq[:], in_=sig[:, :, 2:4], func=ACT.Square, scale=2.0)
             nc.scalar.activation(out=res_ap[:, :, 0:2], in_=sig[:, :, 0:2], func=ACT.Copy, scale=2.0, bias=-0.5)
             live["sq", tagname] = sq
@@ -254,16 +264,18 @@ def tile_head_kernel(tc, f0_bytes, f0_scale, f1, f2, w0, b0, w1, b1, w2, b2, anc
         widen(0, 1, "V")
         widen(0, 2, "V")
         widen(0, 3, "V")
+        widen(1, 0, "S")
+        widen(1, 3, "V")
         w_transposes(0, 0, 2)
         w_transposes(0, 2, 1)
-        interleave0(0, "V")
-        widen(1, 0, "S")
+        interleave0(0, "V", 0, 256)
+        interleave0(0, "V", 256, 512)
         widen(1, 1, "S")
+        widen(1, 2, "S")
         w_empty(0, 0, 2)
         w_empty(0, 2, 1)
-        widen(1, 2, "V")
-        widen(1, 3, "V")
-        quantize(f0q[0], 0, 2048)
+        quantize(f0q[0], 0, 1024)
+        quantize(f0q[0], 1024, 1024)
         quantize(wq[0], 0, 1024)
         quantize(wq[0], 1024, 512)
         bias0_matmul()
@@ -275,39 +287,43 @@ def tile_head_kernel(tc, f0_bytes, f0_scale, f1, f2, w0, b0, w1, b1, w2, b2, anc
         add0(0, 0)
         quantize(f0q[1], 0, 2048)
         matmuls(1, f0q[1], 0)
+        widen(3, 0, "S")
         interleave0(2, "S", 0, 256)
         interleave0(2, "G", 256, 512, "ovA")
         add0(0, 1)
         add0(0, 2)
+        decode0_sigmoid(0)
+        widen(3, 1, "S")
         decode0_scalar(0)
         add0(1, 0)
-        decode0_vector(0)
+        decode0_vector(0, "G")
         store0(0)
         quantize_half(2, 0)
         quantize_half(2, 1)
         w_transposes(1, 0, 2)
         w_transposes(1, 2, 1)
         matmuls(2, f0q[2], 0)
-        for t in range(4):
-            widen(3, t, "S")
+        widen(3, 2, "S")
+        widen(3, 3, "S")
         interleave1(0, "G", "ovA")
-        interleave1(1, "G", "g_f1_1")
         add0(1, 1)
         add0(1, 2)
+        decode0_sigmoid(1)
+        interleave0(3, "S", 0, 256)
+        interleave0(3, "G", 256, 512, "gG_3")
         decode0_scalar(1)
         decode0_vector(1, "G")
         store0(1)
-        interleave0(3, "S", 0, 256)
-        interleave0(3, "G", 256, 512, "gG_3")
         w_transposes(2, 0, 2)
         w_transposes(2, 2, 2)
         w_transposes(2, 4, 2)
+        w_empty(1, 0, 2)
         add0(2, 0)
         add0(2, 1)
         add0(2, 2)
-        decode0_scalar(2)
-        w_empty(1, 0, 2)
+        decode0_sigmoid(2)
         w_empty(1, 2, 1)
+        decode0_scalar(2)
         quantize_half(3, 0)
         quantize_half(3, 1)
         matmuls(3, f0q[3], 0)
@@ -316,30 +332,34 @@ def tile_head_kernel(tc, f0_bytes, f0_scale, f1, f2, w0, b0, w1, b1, w2, b2, anc
         decode0_vector(2)
         store0(2)
         bias12_matmul()
-        interleave1(2, "G", "ovC")
-        interleave2(0, "G")
+        interleave1(1, "G", "ovC")
+        interleave1(2, "G", "g_f1_2")
         interleave1(3, "S", "g_f1_3")
         w_empty(2, 0, 2)
         w_empty(2, 2, 2)
-        w_empty(2, 4, 2)
+        interleave2(0, "S")
         add0(3, 0)
         add0(3, 1)
         add0(3, 2)
+        decode0_sigmoid(3)
+        w_empty(2, 4, 2)
         decode0_scalar(3)
-        for piece in range(4):
+        for piece in (0, 3, 1, 2):
             quantize1(piece)
         matmuls("l1", (None, f1c, f1s), 1)
+        interleave2(1, "V")
         bias12_empty()
         quantize(wq[2], 0, 2048)
-        interleave2(1, "S")
         decode0_vector(3)
         store0(3)
         quantize(wq[2], 2048, 1024)
+        quantize(f2q, 0, 1024)
         for a in range(NA):
             fields_add("l1_%d" % a, live["o", "l1", a], bias1(a, 0, 4))
         for a in range(NA):
+            fields_sigmoid("l1_%d" % a)
+        for a in range(NA):
             fields_scalar("l1_%d" % a, res1[:, a])
-        quantize(f2q, 0, 1024)
         bank2 = psum.tile([P, NA, P], F32, tag="bank", name="o_l2")
         for a in range(NA):
             for g in range(2):
@@ -358,6 +378,7 @@ def tile_head_kernel(tc, f0_bytes, f0_scale, f1, f2, w0, b0, w1, b1, w2, b2, anc
             nc.sync.dma_start(out=out1[a], in_=res1[:, a].rearrange("p (n i) j -> p n (i j)", n=2))
             if a == 1:
                 fields_add("l2", bank2, bias2[:, :, 0:4])
+                fields_sigmoid("l2")
                 fields_scalar("l2", res2)
         nc.vector.tensor_tensor(out=res2[:, :, 4:P], in0=bank2[:, :, 4:P], in1=bias2[:, :, 4:P], op=ALU.add)
         nc.vector.tensor_tensor(out=res2[:, :, 2:4], in0=live["sq", "l2"][:],

@@ -40,25 +40,25 @@ def tile_head_kernel(tc, f0_bytes, f0_scale, f1, f2, w0, b0, w1, b1, w2, b2, anc
         f0v = [f0_bytes[n].rearrange("(p t) h w -> p t (h w)", t=4) for n in range(2)]
         sc = keep.tile([P, 4], F32, name="sc")
         nc.sync.dma_start(out=sc[:], in_=f0_scale[0, :, 0, 0].rearrange("(p t) -> p t", t=4))
-        f0b_00 = [keep.tile([P, 512], U8, name="f0b_00_%d" % t) for t in range(4)]
+        f0b_00 = [keep.tile([P, 512], U8, name="f0b_00_%d" % t, align_bytes=256) for t in range(4)]
         for t in range(4):
             nc.sync.dma_start(out=f0b_00[t][:], in_=f0v[0][:, t, 0:512])
-        f0b_01 = keep.tile([P, 4, 512], U8, name="f0b_01")
+        f0b_01 = keep.tile([P, 4, 512], U8, name="f0b_01", align_bytes=256)
         nc.sync.dma_start(out=f0b_01[:], in_=f0v[0][:, :, 512:1024])
-        w0sb = keep.tile([P, NA, 512], BF16, name="w0sb")
+        w0sb = keep.tile([P, NA, 512], BF16, name="w0sb", align_bytes=256)
         nc.sync.dma_start(out=w0sb[:], in_=w0.rearrange("(a p) k -> p a k", p=P))
-        f0b_1 = keep.tile([P, 4, 1024], U8, name="f0b_1")
+        f0b_1 = keep.tile([P, 4, 1024], U8, name="f0b_1", align_bytes=256)
         nc.sync.dma_start(out=f0b_1[:], in_=f0v[1])
         nc.sync.dma_start(out=brow[0:1, 0:384], in_=b0.unsqueeze(0))
         nc.sync.dma_start(out=brow[0:1, 384:402], in_=anchors.rearrange("(o l) a j -> o (l a j)", o=1))
-        w1sb = keep.tile([P, NA, 512], BF16, name="w1sb")
+        w1sb = keep.tile([P, NA, 512], BF16, name="w1sb", align_bytes=256)
         nc.sync.dma_start(out=w1sb[:], in_=w1.rearrange("(a p) k -> p a k", p=P))
-        f1sb = keep.tile([P, 2, 4, 256], BF16, name="f1sb")
+        f1sb = keep.tile([P, 2, 4, 256], BF16, name="f1sb", align_bytes=256)
         nc.sync.dma_start(out=f1sb[:].rearrange("p n t c -> p n (t c)"),
                           in_=f1.rearrange("n (p t) h w -> p n (t h w)", t=4))
-        w2sb = keep.tile([P, NA, 1024], BF16, name="w2sb")
+        w2sb = keep.tile([P, NA, 1024], BF16, name="w2sb", align_bytes=256)
         nc.sync.dma_start(out=w2sb[:], in_=w2.rearrange("(a p) k -> p a k", p=P))
-        f2sb = keep.tile([P, 2, 2, 4, 64], BF16, name="f2sb")
+        f2sb = keep.tile([P, 2, 2, 4, 64], BF16, name="f2sb", align_bytes=256)
         for n in range(2):
             nc.sync.dma_start(out=f2sb[:, n].rearrange("p g t c -> p g (t c)"),
                               in_=f2[n].rearrange("(g p t) h w -> p g (t h w)", g=2, t=4))
@@ -85,9 +85,9 @@ def tile_head_kernel(tc, f0_bytes, f0_scale, f1, f2, w0, b0, w1, b1, w2, b2, anc
         f1c = keep.tile([P, 512], U32, name="c_f1", align_bytes=64)
         f1s = keep.tile([P, 512], U8, name="s_f1", align_bytes=64)
         f2q = mx_tiles(1024, "f2")
-        res0 = [keep.tile([P, NA, 4, P], F32, name="res0_%d" % k) for k in range(4)]
-        res1 = keep.tile([P, NA, 4, P], F32, name="res1")
-        res2 = keep.tile([P, NA, P], F32, name="res2")
+        res0 = [keep.tile([P, NA, 4, P], F32, name="res0_%d" % k, align_bytes=256) for k in range(4)]
+        res1 = keep.tile([P, NA, 4, P], F32, name="res1", align_bytes=256)
+        res2 = keep.tile([P, NA, P], F32, name="res2", align_bytes=256)
         live = {}
 
         def widen(k, t, eng):

@@ -16,8 +16,6 @@ P = 128
 NA = 3
 FLOPS = 2 * 384 * (512 * 2048 + 512 * 512 + 1024 * 128)
 
-PERM = [False, False, False, False]
-
 
 def tile_head_kernel(tc, f0_bytes, f0_scale, f1, f2, w0, b0, w1, b1, w2, b2, anchors, out):
     nc = tc.nc
@@ -137,19 +135,16 @@ def tile_head_kernel(tc, f0_bytes, f0_scale, f1, f2, w0, b0, w1, b1, w2, b2, anc
             cols = slice(piece * P, (piece + 1) * P)
             quantize((live["g_f1", piece], f1c[:, cols], f1s[:, cols]), 0, 512)
 
-        def interleave2(g, eng):
-            if eng == "S":
-                nc.scalar.copy(out=f2q[0][:, g * 512:(g + 1) * 512].rearrange("p (n c t) -> p n c t", n=2, t=4),
-                               in_=f2sb[:, :, g].rearrange("p n t c -> p n c t"))
-            elif eng == "V":
-                nc.vector.tensor_copy(out=f2q[0][:, g * 512:(g + 1) * 512].rearrange("p (n c t) -> p n c t", n=2, t=4),
-                                      in_=f2sb[:, :, g].rearrange("p n t c -> p n c t"))
-            else:
-                for n in range(2):
-                    nc.gpsimd.tensor_scalar(
-                        out=f2q[0][:, g * 512 + n * 256:g * 512 + (n + 1) * 256].rearrange("p (c t) -> p c t", t=4),
-                        in0=f2sb[:, n, g].rearrange("p t c -> p c t"),
-                        scalar1=1.0, scalar2=0.0, op0=ALU.mult, op1=ALU.add)
+        def interleave2(g, eng, ns=(0, 1)):
+            for n in ns:
+                dst = f2q[0][:, g * 512 + n * 256:g * 512 + (n + 1) * 256].rearrange("p (c t) -> p c t", t=4)
+                src = f2sb[:, n, g].rearrange("p t c -> p c t")
+                if eng == "S":
+                    nc.scalar.copy(out=dst, in_=src)
+                elif eng == "V":
+                    nc.vector.tensor_copy(out=dst, in_=src)
+                else:
+                    nc.gpsimd.tensor_scalar(out=dst, in0=src, scalar1=1.0, scalar2=0.0, op0=ALU.mult, op1=ALU.add)
 
         def quantize(q3, c0, wd):
             nc.vector.quantize_mx(out=q3[1][:, c0 // 4:(c0 + wd) // 4].bitcast(FP8X4),
@@ -226,25 +221,20 @@ def tile_head_kernel(tc, f0_bytes, f0_scale, f1, f2, w0, b0, w1, b1, w2, b2, anc
 
         def store0(k):
             n, c = divmod(k, 2)
-            if PERM[k]:
-                nc.sync.dma_start(
-                    out=out[n, 0:3072, :].rearrange("(a c p i) j -> c p a (i j)", a=NA, c=2, p=P, i=4)[c],
-                    in_=res0[k][:].rearrange("p a i j -> p a (i j)"))
-            else:
-                for a in range(NA):
-                    r0 = a * 1024 + c * 512
-                    nc.sync.dma_start(out=out[n, r0:r0 + 512, :].rearrange("(i p) j -> p i j", p=P),
-                                      in_=res0[k][:, a])
+            for a in range(NA):
+                r0 = a * 1024 + c * 512
+                nc.sync.dma_start(out=out[n, r0:r0 + 512, :].rearrange("(i p) j -> p i j", p=P),
+                                  in_=res0[k][:, a])
 
         def fields_add(tagname, bank, bias_ap):
             d4 = keep.tile(list(bias_ap.shape), F32, name="d4_" + tagname)
             nc.vector.tensor_tensor(out=d4[:], in0=bank[:, :, 0:4], in1=bias_ap, op=ALU.add)
-            live["d4", tagname] = d4
+            live["d4", tagname] = d4[:]
 
         def fields_sigmoid(tagname):
             d4 = live["d4", tagname]
             sig = keep.tile([P, d4.shape[1], 4], F32, name="sg_" + tagname)
-            nc.scalar.activation(out=sig[:], in_=d4[:], func=ACT.Sigmoid)
+            nc.scalar.activation(out=sig[:], in_=d4, func=ACT.Sigmoid)
             live["sg", tagname] = sig
 
         def fields_scalar(tagname, res_ap):
@@ -256,6 +246,30 @@ def tile_head_kernel(tc, f0_bytes, f0_scale, f1, f2, w0, b0, w1, b1, w2, b2, anc
 
         def bias1(a, j0, j1):
             return bias[:, 384 + a * P + j0:384 + a * P + j1].unsqueeze(1).to_broadcast([P, 4, j1 - j0])
+
+        def add1(a):
+            nc.vector.tensor_tensor(out=res1[:, a], in0=live["o", "l1", a][:], in1=bias1(a, 0, P), op=ALU.add)
+            live["d4", "l1_%d" % a] = res1[:, a, :, 0:4]
+
+        def rest1(a):
+            nc.vector.tensor_tensor(out=res1[:, a, :, 4:P], in0=live["o", "l1", a][:, :, 4:P], in1=bias1(a, 4, P),
+                                    op=ALU.add)
+
+        def copy1(a):
+            raw = keep.tile([P, 4, P - 4], F32, name="raw1_%d" % a)
+            nc.scalar.copy(out=raw[:], in_=live["o", "l1", a][:, :, 4:P])
+            live["raw1", a] = raw
+
+        def bias1_gpsimd(a):
+            nc.gpsimd.tensor_tensor(out=res1[:, a, :, 4:P], in0=live["raw1", a][:], in1=bias1(a, 4, P), op=ALU.add)
+
+        def product1(a, eng="V"):
+            (nc.vector if eng == "V" else nc.gpsimd).tensor_tensor(
+                out=res1[:, a, :, 2:4], in0=live["sq", "l1_%d" % a][:],
+                in1=anc[:, 6 + 2 * a:8 + 2 * a].unsqueeze(1).to_broadcast([P, 4, 2]), op=ALU.mult)
+
+        def store1(a):
+            nc.sync.dma_start(out=out1[a], in_=res1[:, a].rearrange("p (n i) j -> p n (i j)", n=2))
 
         bias2 = bias[:, 768:1152].rearrange("p (a j) -> p a j", a=NA)
         out1 = out[:, 3072:3840, :].rearrange("n (a p i) j -> a p n (i j)", a=NA, i=2)
@@ -312,8 +326,6 @@ def tile_head_kernel(tc, f0_bytes, f0_scale, f1, f2, w0, b0, w1, b1, w2, b2, anc
         interleave0(3, "S", 0, 256)
         interleave0(3, "G", 256, 512, "gG_3")
         decode0_scalar(1)
-        decode0_vector(1, "G")
-        store0(1)
         w_transposes(2, 0, 2)
         w_transposes(2, 2, 2)
         w_transposes(2, 4, 2)
@@ -324,6 +336,8 @@ def tile_head_kernel(tc, f0_bytes, f0_scale, f1, f2, w0, b0, w1, b1, w2, b2, anc
         decode0_sigmoid(2)
         w_empty(1, 2, 1)
         decode0_scalar(2)
+        decode0_vector(1)
+        store0(1)
         quantize_half(3, 0)
         quantize_half(3, 1)
         matmuls(3, f0q[3], 0)
@@ -337,29 +351,24 @@ def tile_head_kernel(tc, f0_bytes, f0_scale, f1, f2, w0, b0, w1, b1, w2, b2, anc
         interleave1(3, "S", "g_f1_3")
         w_empty(2, 0, 2)
         w_empty(2, 2, 2)
-        interleave2(0, "S")
+        interleave2(0, "S", (0,))
         add0(3, 0)
         add0(3, 1)
         add0(3, 2)
         decode0_sigmoid(3)
-        w_empty(2, 4, 2)
+        interleave2(0, "S", (1,))
         decode0_scalar(3)
+        w_empty(2, 4, 2)
         for piece in (0, 3, 1, 2):
             quantize1(piece)
         matmuls("l1", (None, f1c, f1s), 1)
         interleave2(1, "V")
         bias12_empty()
-        quantize(wq[2], 0, 2048)
         decode0_vector(3)
         store0(3)
+        quantize(wq[2], 0, 2048)
         quantize(wq[2], 2048, 1024)
         quantize(f2q, 0, 1024)
-        for a in range(NA):
-            fields_add("l1_%d" % a, live["o", "l1", a], bias1(a, 0, 4))
-        for a in range(NA):
-            fields_sigmoid("l1_%d" % a)
-        for a in range(NA):
-            fields_scalar("l1_%d" % a, res1[:, a])
         bank2 = psum.tile([P, NA, P], F32, tag="bank", name="o_l2")
         for a in range(NA):
             for g in range(2):
@@ -370,16 +379,26 @@ def tile_head_kernel(tc, f0_bytes, f0_scale, f1, f2, w0, b0, w1, b1, w2, b2, anc
                                     rhs=wq[2][1][:, q * P:(q + 1) * P].bitcast(FP8X4),
                                     rhs_scale=wq[2][2][:, q * P:(q + 1) * P],
                                     start=(g == 0), stop=(g == 1))
+        copy1(0)
+        fields_add("l1_0", live["o", "l1", 0], bias1(0, 0, 4))
+        bias1_gpsimd(0)
+        fields_add("l1_1", live["o", "l1", 1], bias1(1, 0, 4))
+        fields_add("l1_2", live["o", "l1", 2], bias1(2, 0, 4))
         for a in range(NA):
-            nc.vector.tensor_tensor(out=res1[:, a, :, 4:P], in0=live["o", "l1", a][:, :, 4:P], in1=bias1(a, 4, P),
-                                    op=ALU.add)
-            nc.vector.tensor_tensor(out=res1[:, a, :, 2:4], in0=live["sq", "l1_%d" % a][:],
-                                    in1=anc[:, 6 + 2 * a:8 + 2 * a].unsqueeze(1).to_broadcast([P, 4, 2]), op=ALU.mult)
-            nc.sync.dma_start(out=out1[a], in_=res1[:, a].rearrange("p (n i) j -> p n (i j)", n=2))
-            if a == 1:
-                fields_add("l2", bank2, bias2[:, :, 0:4])
-                fields_sigmoid("l2")
-                fields_scalar("l2", res2)
+            fields_sigmoid("l1_%d" % a)
+        for a in range(NA):
+            fields_scalar("l1_%d" % a, res1[:, a])
+        rest1(1)
+        fields_add("l2", bank2, bias2[:, :, 0:4])
+        product1(1)
+        store1(1)
+        product1(0, "G")
+        fields_sigmoid("l2")
+        fields_scalar("l2", res2)
+        store1(0)
+        rest1(2)
+        product1(2)
+        store1(2)
         nc.vector.tensor_tensor(out=res2[:, :, 4:P], in0=bank2[:, :, 4:P], in1=bias2[:, :, 4:P], op=ALU.add)
         nc.vector.tensor_tensor(out=res2[:, :, 2:4], in0=live["sq", "l2"][:],
                                 in1=anc[:, 12:18].rearrange("p (a j) -> p a j", j=2), op=ALU.mult)

from contextlib import ExitStack

import concourse.mybir as mybir
from concourse.masks import make_identity

F32 = mybir.dt.float32
BF16 = mybir.dt.bfloat16
U32 = mybir.dt.uint32
U8 = mybir.dt.uint8
FP8 = mybir.dt.float8_e4m3fn
FP8X4 = mybir.dt.float8_e4m3fn_x4
ACT = mybir.ActivationFunctionType
ALU = mybir.AluOpType

P = 128
NA = 3
FLOPS = 2 * 384 * (512 * 2048 + 512 * 512 + 1024 * 128)


def tile_head_kernel(tc, f0_bytes, f0_scale, f1, f2, w0, b0, w1, b1, w2, b2, anchors, out):
    nc = tc.nc
    with ExitStack() as ctx:
        keep = ctx.enter_context(tc.tile_pool(name="keep", bufs=1))
        psum = ctx.enter_context(tc.psum_pool(name="psum", bufs=8))
        ctx.enter_context(tc.manual_schedule())

        zero1 = keep.tile([P, 1], F32, name="zero1")
        nc.vector.memset(zero1[:], 0.0)
        warm = keep.tile([P, 1], F32, name="warm")
        nc.scalar.activation(out=warm[:], in_=zero1[:], func=ACT.Sigmoid)
        ident = keep.tile([P, P], F32, name="ident")
        make_identity(nc, ident[:])
        ones = keep.tile([P, P], BF16, name="ones")
        nc.vector.memset(ones[:], 1.0)
        brow = keep.tile([P, 1184], BF16, name="brow")
        nc.vector.memset(brow[:], 0.0)

        f0v = [f0_bytes[n].rearrange("(p t) h w -> p t (h w)", t=4) for n in range(2)]
        sc = keep.tile([P, 4], F32, name="sc")
        nc.sync.dma_start(out=sc[:], in_=f0_scale[0, :, 0, 0].rearrange("(p t) -> p t", t=4))
        f0b_00 = [keep.tile([P, 512], U8, name="f0b_00_%d" % t, align_bytes=256) for t in range(4)]
        for t in range(4):
            nc.sync.dma_start(out=f0b_00[t][:], in_=f0v[0][:, t, 0:512])
        f0b_01 = keep.tile([P, 4, 512], U8, name="f0b_01", align_bytes=256)
        nc.sync.dma_start(out=f0b_01[:], in_=f0v[0][:, :, 512:1024])
        w0sb = keep.tile([P, NA, 512], BF16, name="w0sb", align_bytes=256)
        nc.sync.dma_start(out=w0sb[:], in_=w0.rearrange("(a p) k -> p a k", p=P))
        f0b_1 = keep.tile([P, 4, 1024], U8, name="f0b_1", align_bytes=256)
        nc.sync.dma_start(out=f0b_1[:], in_=f0v[1])
        nc.sync.dma_start(out=brow[0:1, 0:384], in_=b0.unsqueeze(0))
        nc.sync.dma_start(out=brow[0:1, 384:402], in_=anchors.rearrange("(o l) a j -> o (l a j)", o=1))
        w1sb = keep.tile([P, NA, 512], BF16, name="w1sb", align_bytes=256)
        nc.sync.dma_start(out=w1sb[:], in_=w1.rearrange("(a p) k -> p a k", p=P))
        f1sb = keep.tile([P, 2, 4, 256], BF16, name="f1sb", align_bytes=256)
        nc.sync.dma_start(out=f1sb[:].rearrange("p n t c -> p n (t c)"),
                          in_=f1.rearrange("n (p t) h w -> p n (t h w)", t=4))
        w2sb = keep.tile([P, NA, 1024], BF16, name="w2sb", align_bytes=256)
        nc.sync.dma_start(out=w2sb[:], in_=w2.rearrange("(a p) k -> p a k", p=P))
        f2sb = keep.tile([P, 2, 2, 4, 64], BF16, name="f2sb", align_bytes=256)
        for n in range(2):
            nc.sync.dma_start(out=f2sb[:, n].rearrange("p g t c -> p g (t c)"),
                              in_=f2[n].rearrange("(g p t) h w -> p g (t h w)", g=2, t=4))
        nc.sync.dma_start(out=brow[0:1, 416:800], in_=b1.unsqueeze(0))
        nc.sync.dma_start(out=brow[0:1, 800:1184], in_=b2.unsqueeze(0))
        byte_src = [[f0b_00[t][:] for t in range(4)],
                    [f0b_01[:, t, :] for t in range(4)],
                    [f0b_1[:, t, 0:512] for t in range(4)],
                    [f0b_1[:, t, 512:1024] for t in range(4)]]

        bias = keep.tile([P, 1152], BF16, name="bias")
        anc = keep.tile([P, 18], F32, name="anc")

        def mx_tiles(width, tagname, gtag=None):
            grouped = keep.tile([P, width], BF16, name="g_" + tagname, tag=(gtag or "g_" + tagname), align_bytes=64)
            codes = keep.tile([P, width // 4], U32, name="c_" + tagname, align_bytes=64)
            scales = keep.tile([P, width // 4], U8, name="s_" + tagname, align_bytes=64)
            return grouped, codes, scales

        wq = [mx_tiles(1536, "w0"), mx_tiles(1536, "w1"), mx_tiles(3072, "w2")]
        wsb = [w0sb, w1sb, w2sb]
        wide = [keep.tile([P, 4, 512], BF16, name="wide%d" % k) for k in range(4)]
        f0q = [mx_tiles(2048, "f0_%d" % k, [None, "ovA", None, None][k]) for k in range(4)]
        f1c = keep.tile([P, 512], U32, name="c_f1", align_bytes=64)
        f1s = keep.tile([P, 512], U8, name="s_f1", align_bytes=64)
        f2q = mx_tiles(1024, "f2")
        res0 = [keep.tile([P, NA, 4, P], F32, name="res0_%d" % k, align_bytes=256) for k in range(4)]
        res1 = keep.tile([P, NA, 4, P], F32, name="res1", align_bytes=256)
        res2 = keep.tile([P, NA, P], F32, name="res2", align_bytes=256)
        live = {}

        def widen(k, t, eng):
            src = byte_src[k][t].bitcast(FP8)
            if eng == "S":
                nc.scalar.activation(out=wide[k][:, t, :], in_=src, func=ACT.Copy, scale=sc[:, t:t + 1])
            else:
                nc.vector.tensor_scalar(out=wide[k][:, t, :], in0=src, scalar1=sc[:, t:t + 1], scalar2=None,
                                        op0=ALU.mult)

        def interleave0(k, eng, c0=0, c1=512, tagname=None):
            if tagname is None:
                g = f0q[k][0][:, 4 * c0:4 * c1]
            else:
                gt = keep.tile([P, 4 * (c1 - c0)], BF16, name="gG_%d" % k, tag=tagname, align_bytes=64)
                live["gG", k] = gt
                g = gt[:]
            if eng == "G":
                nc.gpsimd.tensor_scalar(out=g.rearrange("p (m t) -> p m t", t=4),
                                        in0=wide[k][:, :, c0:c1].rearrange("p t m -> p m t"),
                                        scalar1=1.0, scalar2=0.0, op0=ALU.mult, op1=ALU.add)
                return
            dst = g.rearrange("p (c i t) -> p c t i", i=4, t=4)
            src = wide[k][:, :, c0:c1].rearrange("p t (c i) -> p c t i", i=4)
            if eng == "V":
                nc.vector.tensor_copy(out=dst, in_=src)
            else:
                nc.scalar.copy(out=dst, in_=src)

        def quantize_half(k, half):
            src = f0q[k][0][:, 0:1024] if half == 0 else live["gG", k][:]
            nc.vector.quantize_mx(out=f0q[k][1][:, half * 256:(half + 1) * 256].bitcast(FP8X4),
                                  scales=f0q[k][2][:, half * 256:(half + 1) * 256], in_=src)

        def interleave1(piece, eng, tagname):
            n, i = divmod(piece, 2)
            g = keep.tile([P, 512], BF16, name="g_f1_%d" % piece, tag=tagname, align_bytes=64)
            dst = g[:].rearrange("p (m t) -> p m t", t=4)
            src = f1sb[:, n].rearrange("p t (m i) -> p i m t", i=2)[:, i]
            if eng == "G":
                nc.gpsimd.tensor_scalar(out=dst, in0=src, scalar1=1.0, scalar2=0.0, op0=ALU.mult, op1=ALU.add)
            else:
                nc.scalar.copy(out=dst, in_=src)
            live["g_f1", piece] = g

        def quantize1(piece):
            cols = slice(piece * P, (piece + 1) * P)
            quantize((live["g_f1", piece], f1c[:, cols], f1s[:, cols]), 0, 512)

        def interleave2(g, eng, ns=(0, 1)):
            for n in ns:
                dst = f2q[0][:, g * 512 + n * 256:g * 512 + (n + 1) * 256].rearrange("p (c t) -> p c t", t=4)
                src = f2sb[:, n, g].rearrange("p t c -> p c t")
                if eng == "S":
                    nc.scalar.copy(out=dst, in_=src)
                elif eng == "V":
                    nc.vector.tensor_copy(out=dst, in_=src)
                else:
                    nc.gpsimd.tensor_scalar(out=dst, in0=src, scalar1=1.0, scalar2=0.0, op0=ALU.mult, op1=ALU.add)

        def quantize(q3, c0, wd):
            nc.vector.quantize_mx(out=q3[1][:, c0 // 4:(c0 + wd) // 4].bitcast(FP8X4),
                                  scales=q3[2][:, c0 // 4:(c0 + wd) // 4],
                                  in_=q3[0][:, c0:c0 + wd])

        def w_transposes(level, first, n):
            words = wsb[level][:].bitcast(F32)
            bank = psum.tile([P, 2, 2, P], F32, tag="bank", name="wt_%d_%d" % (level, first))
            for s in range(n):
                g, a = divmod(first + s, NA)
                for u in range(2):
                    nc.tensor.transpose(bank[:, s, u, :], words[:, a, 256 * g + u:256 * (g + 1):2], ident[:])
            live["wt", level, first] = bank

        def w_empty(level, first, n):
            bank = live["wt", level, first]
            nc.scalar.copy(
                out=wq[level][0][:, first * 512:(first + n) * 512].bitcast(F32).rearrange(
                    "p (s o u) -> p s o u", s=n, u=2),
                in_=bank[:, 0:n].rearrange("p s u o -> p s o u"))

        def bias0_matmul():
            bb = psum.tile([P, 1024], BF16, tag="bank", name="bb0")
            nc.tensor.matmul(out=bb[:, 0:402], lhsT=ones[:], rhs=brow[:, 0:402], start=True, stop=True)
            live["bb0"] = bb

        def bias0_empty():
            nc.scalar.copy(out=bias[:, 0:384], in_=live["bb0"][:, 0:384])
            nc.scalar.copy(out=anc[:], in_=live["bb0"][:, 384:402])

        def bias12_matmul():
            bb = psum.tile([P, 1024], BF16, tag="bank", name="bb1")
            nc.tensor.matmul(out=bb[:, 0:384], lhsT=ones[:], rhs=brow[:, 416:800], start=True, stop=True)
            nc.tensor.matmul(out=bb[:, 384:768], lhsT=ones[:], rhs=brow[:, 800:1184], start=True, stop=True)
            live["bb1"] = bb

        def bias12_empty():
            nc.scalar.copy(out=bias[:, 384:1152], in_=live["bb1"][:, 0:768])

        def matmuls(tagname, fq, level):
            for a in range(NA):
                bank = psum.tile([P, 4, P], F32, tag="bank", name="o_%s_%d" % (tagname, a))
                for i in range(4):
                    nc.tensor.matmul_mx(out=bank[:, i, :],
                                        lhsT=fq[1][:, i * P:(i + 1) * P].bitcast(FP8X4),
                                        lhsT_scale=fq[2][:, i * P:(i + 1) * P],
                                        rhs=wq[level][1][:, a * P:(a + 1) * P].bitcast(FP8X4),
                                        rhs_scale=wq[level][2][:, a * P:(a + 1) * P],
                                        start=True, stop=True)
                live["o", tagname, a] = bank

        def add0(k, a):
            nc.vector.tensor_tensor(out=res0[k][:, a], in0=live["o", k, a][:],
                                    in1=bias[:, a * P:(a + 1) * P].unsqueeze(1).to_broadcast([P, 4, P]), op=ALU.add)

        def decode0_sigmoid(k):
            sig = keep.tile([P, NA, 4, 4], F32, name="sig0_%d" % k)
            nc.scalar.activation(out=sig[:], in_=res0[k][:, :, :, 0:4], func=ACT.Sigmoid)
            live["sig", k] = sig

        def decode0_scalar(k):
            sig = live["sig", k]
            sq = keep.tile([P, NA, 4, 2], F32, name="sq0_%d" % k, tag=("ovC" if k == 2 else "sq0_%d" % k), align_bytes=64)
            nc.scalar.activation(out=sq[:], in_=sig[:, :, :, 2:4], func=ACT.Square, scale=2.0)
            nc.scalar.activation(out=res0[k][:, :, :, 0:2], in_=sig[:, :, :, 0:2], func=ACT.Copy, scale=2.0, bias=-0.5)
            live["sq", k] = sq

        def decode0_vector(k, eng="V"):
            (nc.vector if eng == "V" else nc.gpsimd).tensor_tensor(
                out=res0[k][:, :, :, 2:4], in0=live["sq", k][:],
                in1=anc[:, 0:6].rearrange("p (a j) -> p a j", j=2).unsqueeze(2).to_broadcast([P, NA, 4, 2]),
                op=ALU.mult)

        def store0(k):
            n, c = divmod(k, 2)
            for a in range(NA):
                r0 = a * 1024 + c * 512
                nc.sync.dma_start(out=out[n, r0:r0 + 512, :].rearrange("(i p) j -> p i j", p=P),
                                  in_=res0[k][:, a])

        def fields_add(tagname, bank, bias_ap):
            d4 = keep.tile(list(bias_ap.shape), F32, name="d4_" + tagname)
            nc.vector.tensor_tensor(out=d4[:], in0=bank[:, :, 0:4], in1=bias_ap, op=ALU.add)
            live["d4", tagname] = d4[:]

        def fields_sigmoid(tagname):
            d4 = live["d4", tagname]
            sig = keep.tile([P, d4.shape[1], 4], F32, name="sg_" + tagname)
            nc.scalar.activation(out=sig[:], in_=d4, func=ACT.Sigmoid)
            live["sg", tagname] = sig

        def fields_scalar(tagname, res_ap):
            sig = live["sg", tagname]
            sq = keep.tile([P, sig.shape[1], 2], F32, name="sq_" + tagname)
            nc.scalar.activation(out=sq[:], in_=sig[:, :, 2:4], func=ACT.Square, scale=2.0)
            nc.scalar.activation(out=res_ap[:, :, 0:2], in_=sig[:, :, 0:2], func=ACT.Copy, scale=2.0, bias=-0.5)
            live["sq", tagname] = sq

        def bias1(a, j0, j1):
            return bias[:, 384 + a * P + j0:384 + a * P + j1].unsqueeze(1).to_broadcast([P, 4, j1 - j0])

        def add1(a):
            nc.vector.tensor_tensor(out=res1[:, a], in0=live["o", "l1", a][:], in1=bias1(a, 0, P), op=ALU.add)
            live["d4", "l1_%d" % a] = res1[:, a, :, 0:4]

        def rest1(a):
            nc.vector.tensor_tensor(out=res1[:, a, :, 4:P], in0=live["o", "l1", a][:, :, 4:P], in1=bias1(a, 4, P),
                                    op=ALU.add)

        def copy1(a):
            raw = keep.tile([P, 4, P - 4], F32, name="raw1_%d" % a)
            nc.scalar.copy(out=raw[:], in_=live["o", "l1", a][:, :, 4:P])
            live["raw1", a] = raw

        def bias1_gpsimd(a):
            nc.gpsimd.tensor_tensor(out=res1[:, a, :, 4:P], in0=live["raw1", a][:], in1=bias1(a, 4, P), op=ALU.add)

        def product1(a, eng="V"):
            (nc.vector if eng == "V" else nc.gpsimd).tensor_tensor(
                out=res1[:, a, :, 2:4], in0=live["sq", "l1_%d" % a][:],
                in1=anc[:, 6 + 2 * a:8 + 2 * a].unsqueeze(1).to_broadcast([P, 4, 2]), op=ALU.mult)

        def store1(a):
            nc.sync.dma_start(out=out1[a], in_=res1[:, a].rearrange("p (n i) j -> p n (i j)", n=2))

        bias2 = bias[:, 768:1152].rearrange("p (a j) -> p a j", a=NA)
        out1 = out[:, 3072:3840, :].rearrange("n (a p i) j -> a p n (i j)", a=NA, i=2)

        widen(0, 0, "S")
        widen(0, 1, "V")
        widen(0, 2, "V")
        widen(0, 3, "V")
        widen(1, 0, "S")
        widen(1, 3, "V")
        w_transposes(0, 0, 2)
        w_transposes(0, 2, 1)
        interleave0(0, "V", 0, 256)
        interleave0(0, "V", 256, 512)
        widen(1, 1, "S")
        widen(1, 2, "S")
        w_empty(0, 0, 2)
        w_empty(0, 2, 1)
        quantize(f0q[0], 0, 1024)
        quantize(f0q[0], 1024, 1024)
        quantize(wq[0], 0, 1024)
        quantize(wq[0], 1024, 512)
        bias0_matmul()
        bias0_empty()
        matmuls(0, f0q[0], 0)
        for t in range(4):
            widen(2, t, "S")
        interleave0(1, "V")
        add0(0, 0)
        quantize(f0q[1], 0, 2048)
        matmuls(1, f0q[1], 0)
        widen(3, 0, "S")
        interleave0(2, "S", 0, 256)
        interleave0(2, "G", 256, 512, "ovA")
        add0(0, 1)
        add0(0, 2)
        decode0_sigmoid(0)
        widen(3, 1, "S")
        decode0_scalar(0)
        add0(1, 0)
        decode0_vector(0, "G")
        store0(0)
        quantize_half(2, 0)
        quantize_half(2, 1)
        w_transposes(1, 0, 2)
        w_transposes(1, 2, 1)
        matmuls(2, f0q[2], 0)
        widen(3, 2, "S")
        widen(3, 3, "S")
        interleave1(0, "G", "ovA")
        add0(1, 1)
        add0(1, 2)
        decode0_sigmoid(1)
        interleave0(3, "S", 0, 256)
        interleave0(3, "G", 256, 512, "gG_3")
        decode0_scalar(1)
        w_transposes(2, 0, 2)
        w_transposes(2, 2, 2)
        w_transposes(2, 4, 2)
        w_empty(1, 0, 2)
        add0(2, 0)
        add0(2, 1)
        add0(2, 2)
        decode0_sigmoid(2)
        w_empty(1, 2, 1)
        decode0_scalar(2)
        decode0_vector(1)
        store0(1)
        quantize_half(3, 0)
        quantize_half(3, 1)
        matmuls(3, f0q[3], 0)
        quantize(wq[1], 0, 1024)
        quantize(wq[1], 1024, 512)
        decode0_vector(2)
        store0(2)
        bias12_matmul()
        interleave1(1, "G", "ovC")
        interleave1(2, "G", "g_f1_2")
        interleave1(3, "S", "g_f1_3")
        w_empty(2, 0, 2)
        w_empty(2, 2, 2)
        interleave2(0, "S", (0,))
        add0(3, 0)
        add0(3, 1)
        add0(3, 2)
        decode0_sigmoid(3)
        interleave2(0, "S", (1,))
        decode0_scalar(3)
        w_empty(2, 4, 2)
        for piece in (0, 3, 1, 2):
            quantize1(piece)
        matmuls("l1", (None, f1c, f1s), 1)
        interleave2(1, "V")
        bias12_empty()
        decode0_vector(3)
        store0(3)
        quantize(wq[2], 0, 2048)
        quantize(wq[2], 2048, 1024)
        quantize(f2q, 0, 1024)
        bank2 = psum.tile([P, NA, P], F32, tag="bank", name="o_l2")
        for a in range(NA):
            for g in range(2):
                q = g * NA + a
                nc.tensor.matmul_mx(out=bank2[:, a, :],
                                    lhsT=f2q[1][:, g * P:(g + 1) * P].bitcast(FP8X4),
                                    lhsT_scale=f2q[2][:, g * P:(g + 1) * P],
                                    rhs=wq[2][1][:, q * P:(q + 1) * P].bitcast(FP8X4),
                                    rhs_scale=wq[2][2][:, q * P:(q + 1) * P],
                                    start=(g == 0), stop=(g == 1))
        copy1(0)
        fields_add("l1_0", live["o", "l1", 0], bias1(0, 0, 4))
        bias1_gpsimd(0)
        fields_add("l1_1", live["o", "l1", 1], bias1(1, 0, 4))
        fields_add("l1_2", live["o", "l1", 2], bias1(2, 0, 4))
        for a in range(NA):
            fields_sigmoid("l1_%d" % a)
        for a in range(NA):
            fields_scalar("l1_%d" % a, res1[:, a])
        rest1(1)
        fields_add("l2", bank2, bias2[:, :, 0:4])
        product1(1)
        store1(1)
        product1(0, "G")
        fields_sigmoid("l2")
        fields_scalar("l2", res2)
        store1(0)
        rest1(2)
        product1(2)
        store1(2)
        nc.vector.tensor_tensor(out=res2[:, :, 4:P], in0=bank2[:, :, 4:P], in1=bias2[:, :, 4:P], op=ALU.add)
        nc.vector.tensor_tensor(out=res2[:, :, 2:4], in0=live["sq", "l2"][:],
                                in1=anc[:, 12:18].rearrange("p (a j) -> p a j", j=2), op=ALU.mult)
        for n in range(2):
            nc.sync.dma_start(out=out[n, 3840:4032, :].rearrange("(a c) j -> c a j", a=NA),
                              in_=res2[n * 64:(n + 1) * 64, :, :])
